import numpy as np
import ml_dtypes


def mxq(x, axis, fmt="e4m3"):
    dtype, down = {"e4m3": (ml_dtypes.float8_e4m3fn, 7), "e5m2": (ml_dtypes.float8_e5m2, 14)}[fmt]
    v = np.moveaxis(np.asarray(x, np.float32).astype(ml_dtypes.bfloat16).astype(np.float64), axis, -1)
    blocks = v.reshape(v.shape[:-1] + (-1, 32))
    amax = np.abs(blocks).max(-1, keepdims=True)
    byte = np.maximum(np.where(amax > 0, np.frexp(amax)[1] - 1 + 127, 0) - down, 1)
    scale = np.exp2(byte - 127.0)
    codes = (blocks / scale).astype(np.float32).astype(dtype).astype(np.float64)
    return np.moveaxis((codes * scale).reshape(v.shape), -1, axis)


WIDE = False


def mx_kscale(k):
    if not WIDE:
        return np.ones(k)
    levels = np.array([10, -10, 5, -5, 0])
    if k % 512:
        return np.exp2(np.random.permutation(np.resize(levels, k // 32))).repeat(32)
    a = np.empty((k // 512, 16))
    for p in range(k // 512):
        a[p, :8] = np.random.permutation(np.resize(levels, 8))
        for g in range(8):
            far = levels[np.abs(levels - a[p, g]) >= 10]
            a[p, g + 8] = far[np.random.randint(len(far))]
    return np.exp2(a.ravel()).repeat(32)


BF16 = ml_dtypes.bfloat16


def bf(x):
    return np.asarray(x, np.float32).astype(BF16)


def f64(x):
    return np.asarray(x).astype(np.float64)


B, S, D, C, M, H = 4, 1024, 512, 16, 512, 4
LN_EPS = 1e-5


def sigmoid(v):
    return 1.0 / (1.0 + np.exp(-v))


def setup_inputs():
    s = mx_kscale(M)
    t = mx_kscale(M)
    u = mx_kscale(M)
    g = np.concatenate([np.ones(D), u])
    return {
        "x": bf(np.random.standard_normal((B, S, D))),
        "query": bf(np.random.standard_normal((B, S, M)) * u),
        "ctx": bf(np.random.standard_normal((B, S, M)) * 0.5 * s),
        "attn_out_w": bf(np.random.standard_normal((M, M)) * 2.0 / np.sqrt(M) * t[:, None] / s[None, :]),
        "attn_out_b": bf(np.random.standard_normal(M) * 0.3 * t),
        "op_w": bf(np.random.standard_normal((D, M)) / np.sqrt(M) / t[None, :]),
        "op_b": bf(np.random.standard_normal(D) * 0.3 + 0.3),
        "gate_w": bf(np.random.standard_normal((D, D + M)) / np.sqrt(D + M) / g[None, :]),
        "gate_b": bf(np.random.standard_normal(D) * 0.5),
        "ln_g": bf(1.0 + 0.1 * np.random.standard_normal(D)),
        "ln_b": bf(0.1 * np.random.standard_normal(D)),
    }


def reference(x, query, ctx, attn_out_w, attn_out_b, op_w, op_b, gate_w, gate_b, ln_g, ln_b):
    x = f64(x)
    r = (mxq(f64(ctx), 2, "e4m3") @ mxq(f64(attn_out_w), 1, "e4m3").T) + f64(attn_out_b)
    retrieved = (mxq(r, 2, "e4m3") @ mxq(f64(op_w), 1, "e4m3").T) + f64(op_b)
    gate_in = np.concatenate([x, f64(query)], axis=-1)
    gate = sigmoid((mxq(gate_in, 2, "e4m3") @ mxq(f64(gate_w), 1, "e4m3").T) + f64(gate_b))
    y = gate * x + (1.0 - gate) * retrieved
    mu = y.mean(axis=-1, keepdims=True)
    var = y.var(axis=-1, keepdims=True)
    return (y - mu) / np.sqrt(var + LN_EPS) * f64(ln_g) + f64(ln_b)

@@ -1,0 +1,398 @@
+from contextlib import ExitStack
+import math
+
+import concourse.mybir as mybir
+from concourse.masks import make_identity
+
+F32 = mybir.dt.float32
+BF16 = mybir.dt.bfloat16
+U32 = mybir.dt.uint32
+U8 = mybir.dt.uint8
+FP8X4 = mybir.dt.float8_e4m3fn_x4
+ALU = mybir.AluOpType
+ACT = mybir.ActivationFunctionType
+
+P = 128
+TOKENS = 4096
+WIDTH = 512
+GROUP = 256
+SUPER = 512
+N_GROUPS = TOKENS // GROUP
+LN_EPS = 1e-5
+FLOPS = 2 * TOKENS * WIDTH * (512 + 512 + 1024)
+
+MANUAL = True
+
+
+def tile_rotelearningmemory_pa_t_kernel(
+    tc, x, query, ctx, attn_out_w, attn_out_b, op_w, op_b, gate_w, gate_b, ln_g, ln_b, out
+):
+    nc = tc.nc
+    x_rows = x.flatten_outer_dims()
+    q_rows = query.flatten_outer_dims()
+    c_rows = ctx.flatten_outer_dims()
+    o_rows = out.flatten_outer_dims()
+
+    with ExitStack() as stack:
+        if MANUAL:
+            stack.enter_context(tc.manual_schedule())
+        const = stack.enter_context(tc.tile_pool(name="const", bufs=1))
+        wtmp = stack.enter_context(tc.tile_pool(name="wtmp", bufs=2))
+        raws = stack.enter_context(tc.tile_pool(name="raws", bufs=3))
+        grps = stack.enter_context(tc.tile_pool(name="grps", bufs=3))
+        cods = stack.enter_context(tc.tile_pool(name="cods", bufs=3))
+        work = stack.enter_context(tc.tile_pool(name="work", bufs=3))
+        stat = stack.enter_context(tc.tile_pool(name="stat", bufs=4))
+        pc = stack.enter_context(tc.psum_pool(name="pc", bufs=1))
+        banks = stack.enter_context(tc.psum_pool(name="banks", bufs=7))
+
+        identf = const.tile([P, P], F32, name="identf")
+        make_identity(nc, identf[:])
+        identb = const.tile([P, P], BF16, name="identb")
+        make_identity(nc, identb[:])
+        mhalf = const.tile([P, 2], F32, name="mhalf")
+        nc.gpsimd.memset(mhalf[:], -0.5)
+        btile = const.tile([P, WIDTH], BF16, name="btile")
+        nc.vector.memset(btile[:], 0.0)
+        junk = const.tile([P, WIDTH], BF16, name="junk")
+
+        for v, vec in enumerate((attn_out_b, op_b, gate_b)):
+            nc.scalar.dma_start(out=btile[v : v + 1, :], in_=vec.rearrange("(o w) -> o w", o=1))
+
+        def load_weight(w, cols, name):
+            raw = const.tile([P, 4, cols], BF16, name=name)
+            nc.sync.dma_start(
+                out=raw[:].rearrange("m t k -> m (t k)"),
+                in_=w.rearrange("(m t) k -> m (t k)", t=4),
+            )
+            return raw
+
+        supers = {}
+        groups = {}
+        for g in range(N_GROUPS):
+            groups[g] = {}
+
+        def load(s):
+            st = {}
+            supers[s] = st
+            rows = slice(s * SUPER, (s + 1) * SUPER)
+            for key, src, bufs in (("c", c_rows, 3), ("x", x_rows, 6), ("q", q_rows, 3)):
+                raw = raws.tile([P, 4, WIDTH], BF16, name="raw%s%d" % (key, s), tag="raw" + key, bufs=bufs)
+                nc.sync.dma_start(out=raw[:], in_=src[rows, :].rearrange("(p j) k -> p j k", j=4))
+                st[key] = raw
+
+        w1raw = load_weight(attn_out_w, 512, "w1raw")
+        load(0)
+        wgraw = load_weight(gate_w, 1024, "wgraw")
+        w2raw = load_weight(op_w, 512, "w2raw")
+
+        lnrow = const.tile([P, 2 * WIDTH], BF16, name="lnrow")
+        nc.vector.memset(lnrow[:], 0.0)
+        nc.scalar.dma_start(out=lnrow[0:1, 0:WIDTH], in_=ln_g.rearrange("(o d) -> o d", o=1))
+        nc.scalar.dma_start(out=lnrow[0:1, WIDTH : 2 * WIDTH], in_=ln_b.rearrange("(o d) -> o d", o=1))
+        ones = const.tile([P, P], BF16, name="ones")
+        nc.vector.memset(ones[:], 1.0)
+        lnbank = pc.tile([P, 2 * WIDTH], BF16, name="lnbank")
+
+        def transposes(bank, src, first, k0):
+            for jj in range(2):
+                words = src[:, first + jj, k0 : k0 + 512].bitcast(F32)
+                for u in range(2):
+                    col = u * 256 + jj * P
+                    nc.tensor.transpose(bank[:, col : col + P], words[:, u : 2 * P : 2], identf[:])
+
+        def leave(on_vector, dst, bank):
+            src = bank[:].rearrange("p (u n) -> p n u", u=2)
+            if on_vector:
+                nc.vector.tensor_copy(out=dst, in_=src)
+            else:
+                nc.scalar.copy(out=dst, in_=src)
+
+        def words_of(grp):
+            return grp[:].bitcast(F32).rearrange("p (n u) -> p n u", u=2)
+
+        def prepare_weight(raw, k0, name):
+            grp = wtmp.tile([P, 2048], BF16, name="g" + name, tag="wgrp", align_bytes=64)
+            for half in range(2):
+                bank = banks.tile([P, 512], F32, name="b%s%d" % (name, half), tag="bank")
+                transposes(bank, raw, 2 * half, k0)
+                leave(True, words_of(grp)[:, half * 256 : (half + 1) * 256, :], bank)
+            codes = const.tile([P, 512], U32, name="c" + name, align_bytes=64)
+            scales = const.tile([P, 512], U8, name="s" + name, align_bytes=64)
+            nc.vector.quantize_mx(out=codes[:].bitcast(FP8X4), scales=scales[:], in_=grp[:])
+            return codes, scales
+
+        bbank = banks.tile([P, 512], F32, name="bbank", tag="bank")
+        for u in range(2):
+            nc.tensor.transpose(bbank[:, u * P : (u + 1) * P], btile[:].bitcast(F32)[:, u : 2 * P : 2], identf[:])
+        bwords = const.tile([P, 8], F32, name="bwords")
+        nc.vector.tensor_copy(
+            out=bwords[:, 0:6].rearrange("p (v u) -> p v u", u=2),
+            in_=bbank[:, 0 : 2 * P].rearrange("p (u v) -> p v u", u=2)[:, 0:3, :],
+        )
+        bias = const.tile([P, 12], F32, name="bias")
+        nc.vector.tensor_copy(out=bias[:], in_=bwords[:, 0:6].bitcast(BF16))
+        nbg = const.tile([P, 4], F32, name="nbg")
+        nc.vector.tensor_scalar(out=nbg[:], in0=bias[:, 8:12], scalar1=-1.0, scalar2=None, op0=ALU.mult)
+
+        weights = {}
+        pairs = {}
+
+        def ok(g):
+            return 0 <= g < N_GROUPS
+
+        def home(g, key):
+            if key == "r" or key == "c":
+                name, bufs, half = ("rc", g if key == "r" else g - 2), 3, (0 if key == "r" else 1)
+            else:
+                name, bufs, half = ("xq", g), 5, (0 if key == "x" else 1)
+            if name not in pairs:
+                pairs[name] = {
+                    "grp": grps.tile(
+                        [P, 8 * GROUP], BF16, name="g%s%d" % (name[0], name[1] + 2), tag="g" + name[0], bufs=bufs,
+                        align_bytes=64,
+                    )
+                }
+            return pairs[name], half
+
+        def grouped(g, key):
+            pair, half = home(g, key)
+            return pair["grp"][:, half * 4 * GROUP : (half + 1) * 4 * GROUP]
+
+        def quantise(name, first, last):
+            pair = pairs[name]
+            label = "%s%d" % (name[0], name[1] + 2)
+            pair["codes"] = cods.tile([P, 2 * GROUP], U32, name="c" + label, tag="c" + name[0], align_bytes=64)
+            pair["scales"] = cods.tile([P, 2 * GROUP], U8, name="s" + label, tag="s" + name[0], align_bytes=64)
+            nc.vector.quantize_mx(
+                out=pair["codes"][:, first * GROUP : last * GROUP].bitcast(FP8X4),
+                scales=pair["scales"][:, first * GROUP : last * GROUP],
+                in_=pair["grp"][:, 4 * first * GROUP : 4 * last * GROUP],
+            )
+
+        def q_rc(t):
+            first = 0 if ok(t) else 1
+            last = 2 if ok(t + 2) else 1
+            if first < last:
+                quantise(("rc", t), first, last)
+
+        def q_xq(g):
+            if ok(g):
+                quantise(("xq", g), 0, 2)
+
+        def ti(g, key):
+            if not ok(g):
+                return
+            bank = banks.tile([P, 512], F32, name="ti%s%d" % (key, g), tag="bank")
+            transposes(bank, supers[g // 2][key], 2 * (g % 2), 0)
+            leave(False, grouped(g, key).bitcast(F32).rearrange("p (n u) -> p n u", u=2), bank)
+
+        def mx(out, wkey, c, g, key, first, count, start, stop):
+            wc, ws = weights[wkey]
+            pair, half = home(g, key)
+            col = slice(c * P, (c + 1) * P)
+            cols = slice(half * GROUP + first, half * GROUP + first + count)
+            nc.tensor.matmul_mx(
+                out=out,
+                lhsT=wc[:, col].bitcast(FP8X4),
+                lhsT_scale=ws[:, col],
+                rhs=pair["codes"][:, cols].bitcast(FP8X4),
+                rhs_scale=pair["scales"][:, cols],
+                start=start,
+                stop=stop,
+            )
+
+        def m1(g, jj):
+            if not ok(g):
+                return
+            bank = banks.tile([P, 512], F32, name="m1_%d_%d" % (g, jj), tag="bank")
+            for c in range(4):
+                mx(bank[:, c * P : (c + 1) * P], "w1", c, g, "c", jj * P, P, True, True)
+            nc.vector.tensor_tensor(
+                out=grouped(g, "r").rearrange("p (n c) -> p n c", c=4)[:, jj * P : (jj + 1) * P, :],
+                in0=bank[:].rearrange("p (c n) -> p n c", c=4),
+                in1=bias[:, 0:4].unsqueeze(1).to_broadcast([P, P, 4]),
+                op=ALU.add,
+            )
+
+        def m3(g, b):
+            if not ok(g):
+                return
+            st = groups[g]
+            if b == 0:
+                st["h"] = work.tile([P, 4, GROUP], F32, name="h%d" % g, tag="h", bufs=4)
+            bank = banks.tile([P, 512], F32, name="m3_%d_%d" % (g, b), tag="bank")
+            for cc in range(2):
+                part = bank[:, cc * GROUP : (cc + 1) * GROUP]
+                mx(part, "wgx", 2 * b + cc, g, "x", 0, GROUP, True, False)
+                mx(part, "wgq", 2 * b + cc, g, "q", 0, GROUP, False, True)
+            for cc in range(2):
+                c = 2 * b + cc
+                nc.scalar.activation(
+                    out=st["h"][:, c, :], in_=bank[:, cc * GROUP : (cc + 1) * GROUP], func=ACT.Sigmoid,
+                    bias=nbg[:, c : c + 1], scale=-1.0,
+                )
+
+        def m2(g, b):
+            if not ok(g):
+                return
+            bank = banks.tile([P, 512], F32, name="m2_%d_%d" % (g, b), tag="bank")
+            groups[g]["m2_%d" % b] = bank
+            for cc in range(2):
+                mx(bank[:, cc * GROUP : (cc + 1) * GROUP], "w2", 2 * b + cc, g, "r", 0, GROUP, True, True)
+
+        def sub(g, b):
+            if not ok(g):
+                return
+            st = groups[g]
+            if b == 0:
+                st["dy"] = work.tile([P, 4, GROUP], F32, name="dy%d" % g, tag="dy", bufs=4)
+            bank = st["m2_%d" % b]
+            for cc in range(2):
+                c = 2 * b + cc
+                nc.vector.scalar_tensor_tensor(
+                    out=st["dy"][:, c, :],
+                    in0=bank[:, cc * GROUP : (cc + 1) * GROUP],
+                    scalar=bias[:, 4 + c : 5 + c],
+                    in1=grouped(g, "x").rearrange("p (n t) -> p n t", t=4)[:, :, c],
+                    op0=ALU.add,
+                    op1=ALU.subtract,
+                )
+
+        def cm(g, jj):
+            if not ok(g):
+                return
+            st = groups[g]
+            tok = slice(jj * P, (jj + 1) * P)
+            nc.gpsimd.tensor_tensor(out=st["dy"][:, :, tok], in0=st["dy"][:, :, tok], in1=st["h"][:, :, tok], op=ALU.mult)
+
+        def tb(g, jj):
+            if not ok(g):
+                return
+            st = groups[g]
+            if jj == 0:
+                st["yc"] = work.tile([P, 2, WIDTH], F32, name="yc%d" % g, tag="yc")
+                for key in ("sums", "nmu", "ssq"):
+                    st[key] = stat.tile([P, 2], F32, name="%s%d" % (key, g), tag=key)
+            bank = banks.tile([P, 512], F32, name="tb%d_%d" % (g, jj), tag="bank")
+            nc.tensor.matmul(
+                out=bank[:].rearrange("p (t m) -> p t m", t=4),
+                lhsT=identb[:],
+                rhs=supers[g // 2]["x"][:, 2 * (g % 2) + jj, :].rearrange("p (m t) -> p t m", t=4),
+                start=True,
+                stop=False,
+            )
+            for c in range(4):
+                nc.tensor.matmul(
+                    out=bank[:, c * P : (c + 1) * P],
+                    lhsT=st["dy"][:, c, jj * P : (jj + 1) * P],
+                    rhs=identf[:],
+                    is_transpose=True,
+                    start=False,
+                    stop=(c == 3),
+                )
+            nc.scalar.activation(
+                out=st["yc"][:, jj, :].rearrange("p (m t) -> p m t", t=4),
+                in_=bank[:].rearrange("p (t m) -> p m t", t=4),
+                func=ACT.Identity,
+                accum_out=st["sums"][:, jj : jj + 1],
+            )
+
+        def mean(g, jj):
+            if not ok(g):
+                return
+            st = groups[g]
+            one = slice(jj, jj + 1)
+            nc.scalar.mul(out=st["nmu"][:, one], in_=st["sums"][:, one], mul=-1.0 / WIDTH)
+
+        def s2(g, jj):
+            if not ok(g):
+                return
+            st = groups[g]
+            one = slice(jj, jj + 1)
+            nc.scalar.activation(
+                out=junk[:], in_=st["yc"][:, jj, :], func=ACT.Square, bias=st["nmu"][:, one], scale=1.0,
+                accum_out=st["ssq"][:, one],
+            )
+
+        def pw(g):
+            if not ok(g):
+                return
+            st = groups[g]
+            st["var"] = stat.tile([P, 2], F32, name="var%d" % g, tag="var")
+            st["rs"] = stat.tile([P, 2], F32, name="rs%d" % g, tag="rs")
+            nc.gpsimd.tensor_scalar(
+                out=st["var"][:], in0=st["ssq"][:], scalar1=1.0 / WIDTH, scalar2=LN_EPS, op0=ALU.mult, op1=ALU.add
+            )
+            nc.gpsimd.tensor_tensor(out=st["rs"][:], in0=st["var"][:], in1=mhalf[:], op=ALU.pow)
+
+        def ln1(g, jj):
+            if not ok(g):
+                return
+            st = groups[g]
+            if jj == 0:
+                st["o"] = work.tile([P, 2, WIDTH], F32, name="o%d" % g, tag="o")
+            nc.vector.scalar_tensor_tensor(
+                out=st["o"][:, jj, :], in0=st["yc"][:, jj, :], scalar=st["nmu"][:, jj : jj + 1], in1=lnbank[:, 0:WIDTH],
+                op0=ALU.add, op1=ALU.mult,
+            )
+
+        def ln2(g, jj):
+            if not ok(g):
+                return
+            st = groups[g]
+            nc.vector.scalar_tensor_tensor(
+                out=st["o"][:, jj, :], in0=st["o"][:, jj, :], scalar=st["rs"][:, jj : jj + 1],
+                in1=lnbank[:, WIDTH : 2 * WIDTH], op0=ALU.mult, op1=ALU.add,
+            )
+            if jj == 1:
+                s = g // 2
+                first = 2 * (g % 2)
+                nc.sync.dma_start(
+                    out=o_rows[s * SUPER : (s + 1) * SUPER, :].rearrange("(p j) d -> p j d", j=4)[:, first : first + 2, :],
+                    in_=st["o"][:],
+                )
+
+        loaded = 1
+        for t in range(-3, N_GROUPS + 4):
+            while loaded < N_GROUPS // 2 and 2 * loaded - 6 <= t:
+                load(loaded)
+                loaded += 1
+            if t == -3:
+                weights["w1"] = prepare_weight(w1raw, 0, "w1")
+            ln1(t - 4, 0)
+            ln1(t - 4, 1)
+            q_rc(t)
+            q_xq(t + 1)
+            if t == -1:
+                weights["wgx"] = prepare_weight(wgraw, 0, "wgx")
+                weights["wgq"] = prepare_weight(wgraw, 512, "wgq")
+            if t == 0:
+                weights["w2"] = prepare_weight(w2raw, 0, "w2")
+            if t == 1:
+                nc.tensor.matmul(out=lnbank[:, 0:WIDTH], lhsT=ones[:], rhs=lnrow[:, 0:WIDTH], start=True, stop=True)
+                nc.tensor.matmul(
+                    out=lnbank[:, WIDTH : 2 * WIDTH], lhsT=ones[:], rhs=lnrow[:, WIDTH : 2 * WIDTH], start=True, stop=True
+                )
+            ti(t + 3, "c")
+            tb(t - 3, 1)
+            mean(t - 3, 0)
+            ti(t + 2, "x")
+            mean(t - 3, 1)
+            s2(t - 3, 0)
+            s2(t - 3, 1)
+            pw(t - 3)
+            m2(t - 1, 0)
+            m2(t - 1, 1)
+            m3(t, 0)
+            m3(t, 1)
+            sub(t - 1, 0)
+            sub(t - 1, 1)
+            cm(t - 1, 0)
+            cm(t - 1, 1)
+            ln2(t - 4, 0)
+            ln2(t - 4, 1)
+            tb(t - 2, 0)
+            ti(t + 2, "q")
+            m1(t + 1, 0)
+            m1(t + 1, 1)

@@ -276,15 +276,15 @@ def tile_rotelearningmemory_pa_t_kernel(
                     st[key] = stat.tile([P, 2], F32, name="%s%d" % (key, g), tag=key)
             bank = banks.tile([P, 512], F32, name="tb%d_%d" % (g, jj), tag="bank")
             nc.tensor.matmul(
-                out=bank[:].rearrange("p (t m) -> p t m", t=4),
+                out=bank[:],
                 lhsT=identb[:],
-                rhs=supers[g // 2]["x"][:, 2 * (g % 2) + jj, :].rearrange("p (m t) -> p t m", t=4),
+                rhs=supers[g // 2]["x"][:, 2 * (g % 2) + jj, :],
                 start=True,
                 stop=False,
             )
             for c in range(4):
                 nc.tensor.matmul(
-                    out=bank[:, c * P : (c + 1) * P],
+                    out=bank[:].rearrange("p (m t) -> p m t", t=4)[:, :, c],
                     lhsT=st["dy"][:, c, jj * P : (jj + 1) * P],
                     rhs=identf[:],
                     is_transpose=True,
@@ -292,8 +292,8 @@ def tile_rotelearningmemory_pa_t_kernel(
                     stop=(c == 3),
                 )
             nc.scalar.activation(
-                out=st["yc"][:, jj, :].rearrange("p (m t) -> p m t", t=4),
-                in_=bank[:].rearrange("p (t m) -> p m t", t=4),
+                out=st["yc"][:, jj, :],
+                in_=bank[:],
                 func=ACT.Identity,
                 accum_out=st["sums"][:, jj : jj + 1],
             )

@@ -180,12 +180,26 @@ def tile_rotelearningmemory_pa_t_kernel(
             if ok(g):
                 quantise(("xq", g), 0, 2)
 
+        def ti_open(g, key):
+            if ok(g):
+                groups[g]["ti" + key] = banks.tile([P, 512], F32, name="ti%s%d" % (key, g), tag="bank")
+
+        def ti_t(g, key, i):
+            if ok(g):
+                jj, u = i // 2, i % 2
+                words = supers[g // 2][key][:, 2 * (g % 2) + jj, :].bitcast(F32)
+                col = u * 256 + jj * P
+                nc.tensor.transpose(groups[g]["ti" + key][:, col : col + P], words[:, u : 2 * P : 2], identf[:])
+
+        def ti_out(g, key):
+            if ok(g):
+                leave(False, grouped(g, key).bitcast(F32).rearrange("p (n u) -> p n u", u=2), groups[g]["ti" + key])
+
         def ti(g, key):
-            if not ok(g):
-                return
-            bank = banks.tile([P, 512], F32, name="ti%s%d" % (key, g), tag="bank")
-            transposes(bank, supers[g // 2][key], 2 * (g % 2), 0)
-            leave(False, grouped(g, key).bitcast(F32).rearrange("p (n u) -> p n u", u=2), bank)
+            ti_open(g, key)
+            for i in range(4):
+                ti_t(g, key, i)
+            ti_out(g, key)
 
         def mx(out, wkey, c, g, key, first, count, start, stop):
             wc, ws = weights[wkey]
@@ -266,7 +280,7 @@ def tile_rotelearningmemory_pa_t_kernel(
             tok = slice(jj * P, (jj + 1) * P)
             nc.gpsimd.tensor_tensor(out=st["dy"][:, :, tok], in0=st["dy"][:, :, tok], in1=st["h"][:, :, tok], op=ALU.mult)
 
-        def tb(g, jj):
+        def tbx(g, jj):
             if not ok(g):
                 return
             st = groups[g]
@@ -275,6 +289,7 @@ def tile_rotelearningmemory_pa_t_kernel(
                 for key in ("sums", "nmu", "ssq"):
                     st[key] = stat.tile([P, 2], F32, name="%s%d" % (key, g), tag=key)
             bank = banks.tile([P, 512], F32, name="tb%d_%d" % (g, jj), tag="bank")
+            st["tb%d" % jj] = bank
             nc.tensor.matmul(
                 out=bank[:],
                 lhsT=identb[:],
@@ -282,7 +297,10 @@ def tile_rotelearningmemory_pa_t_kernel(
                 start=True,
                 stop=False,
             )
-            for c in range(4):
+        def tbt(g, jj, c):
+            if ok(g):
+                st = groups[g]
+                bank = st["tb%d" % jj]
                 nc.tensor.matmul(
                     out=bank[:].rearrange("p (m t) -> p m t", t=4)[:, :, c],
                     lhsT=st["dy"][:, c, jj * P : (jj + 1) * P],
@@ -291,12 +309,22 @@ def tile_rotelearningmemory_pa_t_kernel(
                     start=False,
                     stop=(c == 3),
                 )
+        def tbo(g, jj):
+            if not ok(g):
+                return
+            st = groups[g]
             nc.scalar.activation(
                 out=st["yc"][:, jj, :],
-                in_=bank[:],
+                in_=st["tb%d" % jj][:],
                 func=ACT.Identity,
                 accum_out=st["sums"][:, jj : jj + 1],
             )
+
+        def tb(g, jj):
+            tbx(g, jj)
+            for c in range(4):
+                tbt(g, jj, c)
+            tbo(g, jj)
 
         def mean(g, jj):
             if not ok(g):
@@ -375,9 +403,14 @@ def tile_rotelearningmemory_pa_t_kernel(
                     out=lnbank[:, WIDTH : 2 * WIDTH], lhsT=ones[:], rhs=lnrow[:, WIDTH : 2 * WIDTH], start=True, stop=True
                 )
             ti(t + 3, "c")
-            tb(t - 3, 1)
+            tbx(t - 3, 1)
+            ti_open(t + 2, "x")
+            for i in range(4):
+                tbt(t - 3, 1, i)
+                ti_t(t + 2, "x", i)
+            tbo(t - 3, 1)
             mean(t - 3, 0)
-            ti(t + 2, "x")
+            ti_out(t + 2, "x")
             mean(t - 3, 1)
             s2(t - 3, 0)
             s2(t - 3, 1)
@@ -392,7 +425,12 @@ def tile_rotelearningmemory_pa_t_kernel(
             cm(t - 1, 1)
             ln2(t - 4, 0)
             ln2(t - 4, 1)
-            tb(t - 2, 0)
-            ti(t + 2, "q")
+            tbx(t - 2, 0)
+            ti_open(t + 2, "q")
+            for i in range(4):
+                tbt(t - 2, 0, i)
+                ti_t(t + 2, "q", i)
+            tbo(t - 2, 0)
+            ti_out(t + 2, "q")
             m1(t + 1, 0)
             m1(t + 1, 1)

@@ -1,5 +1,4 @@
 from contextlib import ExitStack
-import math
 
 import concourse.mybir as mybir
 from concourse.masks import make_identity
@@ -15,27 +14,28 @@ ACT = mybir.ActivationFunctionType
 P = 128
 TOKENS = 4096
 WIDTH = 512
-GROUP = 256
 SUPER = 512
-N_GROUPS = TOKENS // GROUP
+N_SUPERS = TOKENS // SUPER
 LN_EPS = 1e-5
 FLOPS = 2 * TOKENS * WIDTH * (512 + 512 + 1024)
-
-MANUAL = True
 
 
 def tile_rotelearningmemory_pa_t_kernel(
     tc, x, query, ctx, attn_out_w, attn_out_b, op_w, op_b, gate_w, gate_b, ln_g, ln_b, out
 ):
     nc = tc.nc
-    x_rows = x.flatten_outer_dims()
-    q_rows = query.flatten_outer_dims()
-    c_rows = ctx.flatten_outer_dims()
+    sources = {"x": x.flatten_outer_dims(), "q": query.flatten_outer_dims(), "c": ctx.flatten_outer_dims()}
     o_rows = out.flatten_outer_dims()
 
+    sizes = [2] * 16
+    plan = []
+    for n in sizes:
+        done = sum(p[2] for p in plan)
+        plan.append((done // 4, done % 4, n))
+    N_GROUPS = len(plan)
+
     with ExitStack() as stack:
-        if MANUAL:
-            stack.enter_context(tc.manual_schedule())
+        stack.enter_context(tc.manual_schedule())
         const = stack.enter_context(tc.tile_pool(name="const", bufs=1))
         wtmp = stack.enter_context(tc.tile_pool(name="wtmp", bufs=2))
         raws = stack.enter_context(tc.tile_pool(name="raws", bufs=3))
@@ -54,38 +54,9 @@ def tile_rotelearningmemory_pa_t_kernel(
         nc.gpsimd.memset(mhalf[:], -0.5)
         btile = const.tile([P, WIDTH], BF16, name="btile")
         nc.vector.memset(btile[:], 0.0)
-        junk = const.tile([P, WIDTH], BF16, name="junk")
-
+        junk = [const.tile([P, WIDTH], BF16, name="junk%d" % i) for i in range(2)]
         for v, vec in enumerate((attn_out_b, op_b, gate_b)):
             nc.scalar.dma_start(out=btile[v : v + 1, :], in_=vec.rearrange("(o w) -> o w", o=1))
-
-        def load_weight(w, cols, name):
-            raw = const.tile([P, 4, cols], BF16, name=name)
-            nc.sync.dma_start(
-                out=raw[:].rearrange("m t k -> m (t k)"),
-                in_=w.rearrange("(m t) k -> m (t k)", t=4),
-            )
-            return raw
-
-        supers = {}
-        groups = {}
-        for g in range(N_GROUPS):
-            groups[g] = {}
-
-        def load(s):
-            st = {}
-            supers[s] = st
-            rows = slice(s * SUPER, (s + 1) * SUPER)
-            for key, src, bufs in (("c", c_rows, 3), ("x", x_rows, 6), ("q", q_rows, 3)):
-                raw = raws.tile([P, 4, WIDTH], BF16, name="raw%s%d" % (key, s), tag="raw" + key, bufs=bufs)
-                nc.sync.dma_start(out=raw[:], in_=src[rows, :].rearrange("(p j) k -> p j k", j=4))
-                st[key] = raw
-
-        w1raw = load_weight(attn_out_w, 512, "w1raw")
-        load(0)
-        wgraw = load_weight(gate_w, 1024, "wgraw")
-        w2raw = load_weight(op_w, 512, "w2raw")
-
         lnrow = const.tile([P, 2 * WIDTH], BF16, name="lnrow")
         nc.vector.memset(lnrow[:], 0.0)
         nc.scalar.dma_start(out=lnrow[0:1, 0:WIDTH], in_=ln_g.rearrange("(o d) -> o d", o=1))
@@ -94,120 +65,181 @@ def tile_rotelearningmemory_pa_t_kernel(
         nc.vector.memset(ones[:], 1.0)
         lnbank = pc.tile([P, 2 * WIDTH], BF16, name="lnbank")
 
-        def transposes(bank, src, first, k0):
-            for jj in range(2):
-                words = src[:, first + jj, k0 : k0 + 512].bitcast(F32)
+        supers = {}
+
+        def alloc(s):
+            supers[s] = {}
+            for key, bufs in (("c", 3), ("x", 6), ("q", 3)):
+                supers[s][key] = raws.tile([P, 4, WIDTH], BF16, name="raw%s%d" % (key, s), tag="raw" + key, bufs=bufs)
+
+        def fetch(s, key, j0, nj):
+            rows = sources[key][s * SUPER : (s + 1) * SUPER, :].rearrange("(p j) k -> p j k", j=4)
+            nc.sync.dma_start(out=supers[s][key][:, j0 : j0 + nj, :], in_=rows[:, j0 : j0 + nj, :])
+
+        def load(s):
+            alloc(s)
+            for key in ("c", "x", "q"):
+                fetch(s, key, 0, 4)
+
+        def load_weight(w, k0, name):
+            raw = const.tile([P, 4, 512], BF16, name=name)
+            src = w.rearrange("(m t) k -> m t k", t=4)[:, :, k0 : k0 + 512]
+            nc.sync.dma_start(out=raw[:], in_=src)
+            return raw
+
+        def transposes(bank, src, first, n):
+            for jj in range(n):
+                words = src[:, first + jj, :].bitcast(F32)
                 for u in range(2):
-                    col = u * 256 + jj * P
+                    col = u * n * P + jj * P
                     nc.tensor.transpose(bank[:, col : col + P], words[:, u : 2 * P : 2], identf[:])
 
         def leave(on_vector, dst, bank):
-            src = bank[:].rearrange("p (u n) -> p n u", u=2)
             if on_vector:
-                nc.vector.tensor_copy(out=dst, in_=src)
+                nc.vector.tensor_copy(out=dst, in_=bank)
             else:
-                nc.scalar.copy(out=dst, in_=src)
+                nc.scalar.copy(out=dst, in_=bank)
 
-        def words_of(grp):
-            return grp[:].bitcast(F32).rearrange("p (n u) -> p n u", u=2)
-
-        def prepare_weight(raw, k0, name):
+        def prepare_weight(raw, name):
             grp = wtmp.tile([P, 2048], BF16, name="g" + name, tag="wgrp", align_bytes=64)
+            words = grp[:].bitcast(F32).rearrange("p (n u) -> p n u", u=2)
             for half in range(2):
                 bank = banks.tile([P, 512], F32, name="b%s%d" % (name, half), tag="bank")
-                transposes(bank, raw, 2 * half, k0)
-                leave(True, words_of(grp)[:, half * 256 : (half + 1) * 256, :], bank)
+                transposes(bank, raw, 2 * half, 2)
+                leave(half == 1, words[:, half * 256 : (half + 1) * 256, :], bank[:].rearrange("p (u n) -> p n u", u=2))
             codes = const.tile([P, 512], U32, name="c" + name, align_bytes=64)
             scales = const.tile([P, 512], U8, name="s" + name, align_bytes=64)
             nc.vector.quantize_mx(out=codes[:].bitcast(FP8X4), scales=scales[:], in_=grp[:])
-            return codes, scales
-
-        bbank = banks.tile([P, 512], F32, name="bbank", tag="bank")
-        for u in range(2):
-            nc.tensor.transpose(bbank[:, u * P : (u + 1) * P], btile[:].bitcast(F32)[:, u : 2 * P : 2], identf[:])
-        bwords = const.tile([P, 8], F32, name="bwords")
-        nc.vector.tensor_copy(
-            out=bwords[:, 0:6].rearrange("p (v u) -> p v u", u=2),
-            in_=bbank[:, 0 : 2 * P].rearrange("p (u v) -> p v u", u=2)[:, 0:3, :],
-        )
-        bias = const.tile([P, 12], F32, name="bias")
-        nc.vector.tensor_copy(out=bias[:], in_=bwords[:, 0:6].bitcast(BF16))
-        nbg = const.tile([P, 4], F32, name="nbg")
-        nc.vector.tensor_scalar(out=nbg[:], in0=bias[:, 8:12], scalar1=-1.0, scalar2=None, op0=ALU.mult)
+            weights[name] = (codes, scales)
 
         weights = {}
+        bias = const.tile([P, 12], F32, name="bias")
+        nbg = const.tile([P, 4], F32, name="nbg")
+
+        def prepare_bias():
+            bbank = banks.tile([P, 512], F32, name="bbank", tag="bank")
+            for u in range(2):
+                nc.tensor.transpose(bbank[:, u * P : (u + 1) * P], btile[:].bitcast(F32)[:, u : 2 * P : 2], identf[:])
+            bwords = const.tile([P, 8], F32, name="bwords")
+            nc.vector.tensor_copy(
+                out=bwords[:, 0:6].rearrange("p (v u) -> p v u", u=2),
+                in_=bbank[:, 0 : 2 * P].rearrange("p (u v) -> p v u", u=2)[:, 0:3, :],
+            )
+            nc.vector.tensor_copy(out=bias[:], in_=bwords[:, 0:6].bitcast(BF16))
+            nc.vector.tensor_scalar(out=nbg[:], in0=bias[:, 8:12], scalar1=-1.0, scalar2=None, op0=ALU.mult)
+
+        def spread_ln():
+            for h in range(2):
+                cols = slice(h * WIDTH, (h + 1) * WIDTH)
+                nc.tensor.matmul(out=lnbank[:, cols], lhsT=ones[:], rhs=lnrow[:, cols], start=True, stop=True)
+
+        groups = [{} for g in range(N_GROUPS)]
         pairs = {}
 
         def ok(g):
             return 0 <= g < N_GROUPS
 
         def home(g, key):
-            if key == "r" or key == "c":
-                name, bufs, half = ("rc", g if key == "r" else g - 2), 3, (0 if key == "r" else 1)
+            if key in ("r", "c"):
+                name, bufs, half = ("rc", g if key == "r" else g - 1), 3, (0 if key == "r" else 1)
             else:
                 name, bufs, half = ("xq", g), 5, (0 if key == "x" else 1)
             if name not in pairs:
                 pairs[name] = {
-                    "grp": grps.tile(
-                        [P, 8 * GROUP], BF16, name="g%s%d" % (name[0], name[1] + 2), tag="g" + name[0], bufs=bufs,
-                        align_bytes=64,
-                    )
+                    "grp": grps.tile([P, 8 * 256], BF16, name="g%s%d" % (name[0], name[1] + 4), tag="g" + name[0], bufs=bufs, align_bytes=64)
                 }
             return pairs[name], half
 
-        def grouped(g, key):
-            pair, half = home(g, key)
-            return pair["grp"][:, half * 4 * GROUP : (half + 1) * 4 * GROUP]
+        def width(g):
+            return plan[g][2] * P
 
-        def quantise(name, first, last):
+        def place(g, key):
+            pair, half = home(g, key)
+            if half == 0:
+                return pair, 0
+            mate = g if key == "q" else g - 1
+            return pair, (width(mate) if ok(mate) else 0)
+
+        def grouped(g, key):
+            pair, col = place(g, key)
+            return pair["grp"][:, 4 * col : 4 * (col + width(g))]
+
+        def quantise(name, cols):
             pair = pairs[name]
-            label = "%s%d" % (name[0], name[1] + 2)
-            pair["codes"] = cods.tile([P, 2 * GROUP], U32, name="c" + label, tag="c" + name[0], align_bytes=64)
-            pair["scales"] = cods.tile([P, 2 * GROUP], U8, name="s" + label, tag="s" + name[0], align_bytes=64)
-            nc.vector.quantize_mx(
-                out=pair["codes"][:, first * GROUP : last * GROUP].bitcast(FP8X4),
-                scales=pair["scales"][:, first * GROUP : last * GROUP],
-                in_=pair["grp"][:, 4 * first * GROUP : 4 * last * GROUP],
-            )
+            label = "%s%d" % (name[0], name[1] + 4)
+            if "codes" not in pair:
+                pair["codes"] = cods.tile([P, 512], U32, name="c" + label, tag="c" + name[0], align_bytes=64)
+                pair["scales"] = cods.tile([P, 512], U8, name="s" + label, tag="s" + name[0], align_bytes=64)
+            while cols[0] < cols[1]:
+                n = cols[1] - cols[0]
+                n = 512 if n >= 512 else (256 if n >= 256 else 128)
+                sl = slice(cols[0], cols[0] + n)
+                nc.vector.quantize_mx(
+                    out=pair["codes"][:, sl].bitcast(FP8X4),
+                    scales=pair["scales"][:, sl],
+                    in_=pair["grp"][:, 4 * cols[0] : 4 * (cols[0] + n)],
+                )
+                cols = (cols[0] + n, cols[1])
+
+        def q_one(g, key):
+            if ok(g):
+                pair, col = place(g, key)
+                quantise(home_name(g, key), (col, col + width(g)))
+
+        def home_name(g, key):
+            return ("rc", g if key == "r" else g - 1) if key in ("r", "c") else ("xq", g)
 
         def q_rc(t):
-            first = 0 if ok(t) else 1
-            last = 2 if ok(t + 2) else 1
-            if first < last:
-                quantise(("rc", t), first, last)
+            first = 0 if ok(t) else None
+            c = t + 1
+            if ok(t) and ok(c):
+                quantise(("rc", t), (0, width(t) + width(c)))
+            elif ok(t):
+                q_one(t, "r")
+            elif ok(c):
+                q_one(c, "c")
 
         def q_xq(g):
             if ok(g):
-                quantise(("xq", g), 0, 2)
+                quantise(("xq", g), (0, 2 * width(g)))
 
         def ti_open(g, key):
             if ok(g):
                 groups[g]["ti" + key] = banks.tile([P, 512], F32, name="ti%s%d" % (key, g), tag="bank")
 
+        def ti_n(g):
+            return 2 * plan[g][2] if ok(g) else 0
+
         def ti_t(g, key, i):
-            if ok(g):
+            if ok(g) and i < ti_n(g):
+                s, j0, nj = plan[g]
                 jj, u = i // 2, i % 2
-                words = supers[g // 2][key][:, 2 * (g % 2) + jj, :].bitcast(F32)
-                col = u * 256 + jj * P
+                words = supers[s][key][:, j0 + jj, :].bitcast(F32)
+                col = u * nj * P + jj * P
                 nc.tensor.transpose(groups[g]["ti" + key][:, col : col + P], words[:, u : 2 * P : 2], identf[:])
 
-        def ti_out(g, key):
+        def ti_out(g, key, on_vector=False):
             if ok(g):
-                leave(False, grouped(g, key).bitcast(F32).rearrange("p (n u) -> p n u", u=2), groups[g]["ti" + key])
+                n = width(g)
+                leave(
+                    on_vector,
+                    grouped(g, key).bitcast(F32).rearrange("p (n u) -> p n u", u=2),
+                    groups[g]["ti" + key][:, 0 : 2 * n].rearrange("p (u n) -> p n u", u=2),
+                )
 
-        def ti(g, key):
+        def ti(g, key, on_vector=False):
             ti_open(g, key)
             for i in range(4):
                 ti_t(g, key, i)
-            ti_out(g, key)
+            ti_out(g, key, on_vector)
 
-        def mx(out, wkey, c, g, key, first, count, start, stop):
+        def mx(dst, wkey, c, g, key, first, count, start, stop):
             wc, ws = weights[wkey]
-            pair, half = home(g, key)
+            pair, at = place(g, key)
             col = slice(c * P, (c + 1) * P)
-            cols = slice(half * GROUP + first, half * GROUP + first + count)
+            cols = slice(at + first, at + first + count)
             nc.tensor.matmul_mx(
-                out=out,
+                out=dst,
                 lhsT=wc[:, col].bitcast(FP8X4),
                 lhsT_scale=ws[:, col],
                 rhs=pair["codes"][:, cols].bitcast(FP8X4),
@@ -216,108 +248,139 @@ def tile_rotelearningmemory_pa_t_kernel(
                 stop=stop,
             )
 
-        def m1(g, jj):
+        def m1(g):
             if not ok(g):
                 return
-            bank = banks.tile([P, 512], F32, name="m1_%d_%d" % (g, jj), tag="bank")
-            for c in range(4):
-                mx(bank[:, c * P : (c + 1) * P], "w1", c, g, "c", jj * P, P, True, True)
-            nc.vector.tensor_tensor(
-                out=grouped(g, "r").rearrange("p (n c) -> p n c", c=4)[:, jj * P : (jj + 1) * P, :],
-                in0=bank[:].rearrange("p (c n) -> p n c", c=4),
-                in1=bias[:, 0:4].unsqueeze(1).to_broadcast([P, P, 4]),
-                op=ALU.add,
-            )
+            for jj in range(plan[g][2]):
+                bank = banks.tile([P, 512], F32, name="m1_%d_%d" % (g, jj), tag="bank")
+                for c in range(4):
+                    mx(bank[:, c * P : (c + 1) * P], "w1", c, g, "c", jj * P, P, True, True)
+                nc.vector.tensor_tensor(
+                    out=grouped(g, "r").rearrange("p (n c) -> p n c", c=4)[:, jj * P : (jj + 1) * P, :],
+                    in0=bank[:].rearrange("p (c n) -> p n c", c=4),
+                    in1=bias[:, 0:4].unsqueeze(1).to_broadcast([P, P, 4]),
+                    op=ALU.add,
+                )
 
-        def m3(g, b):
+        def per_bank(g):
+            return 512 // width(g)
+
+        def m3(g):
             if not ok(g):
                 return
             st = groups[g]
-            if b == 0:
-                st["h"] = work.tile([P, 4, GROUP], F32, name="h%d" % g, tag="h", bufs=4)
-            bank = banks.tile([P, 512], F32, name="m3_%d_%d" % (g, b), tag="bank")
-            for cc in range(2):
-                part = bank[:, cc * GROUP : (cc + 1) * GROUP]
-                mx(part, "wgx", 2 * b + cc, g, "x", 0, GROUP, True, False)
-                mx(part, "wgq", 2 * b + cc, g, "q", 0, GROUP, False, True)
-            for cc in range(2):
-                c = 2 * b + cc
+            n = width(g)
+            st["h"] = work.tile([P, 4, 256], F32, name="h%d" % g, tag="h", bufs=5)
+            st["m3"] = []
+            for b in range(4 // per_bank(g)):
+                bank = banks.tile([P, 512], F32, name="m3_%d_%d" % (g, b), tag="bank")
+                st["m3"].append(bank)
+                for cc in range(per_bank(g)):
+                    part = bank[:, cc * n : (cc + 1) * n]
+                    c = per_bank(g) * b + cc
+                    mx(part, "wgx", c, g, "x", 0, n, True, False)
+                    mx(part, "wgq", c, g, "q", 0, n, False, True)
+
+        def sg(g):
+            if not ok(g):
+                return
+            st = groups[g]
+            n = width(g)
+            for c in range(4):
+                b, cc = c // per_bank(g), c % per_bank(g)
                 nc.scalar.activation(
-                    out=st["h"][:, c, :], in_=bank[:, cc * GROUP : (cc + 1) * GROUP], func=ACT.Sigmoid,
+                    out=st["h"][:, c, 0:n], in_=st["m3"][b][:, cc * n : (cc + 1) * n], func=ACT.Sigmoid,
                     bias=nbg[:, c : c + 1], scale=-1.0,
                 )
 
-        def m2(g, b):
+        def m2(g):
             if not ok(g):
                 return
-            bank = banks.tile([P, 512], F32, name="m2_%d_%d" % (g, b), tag="bank")
-            groups[g]["m2_%d" % b] = bank
-            for cc in range(2):
-                mx(bank[:, cc * GROUP : (cc + 1) * GROUP], "w2", 2 * b + cc, g, "r", 0, GROUP, True, True)
+            n = width(g)
+            groups[g]["m2"] = []
+            for b in range(4 // per_bank(g)):
+                bank = banks.tile([P, 512], F32, name="m2_%d_%d" % (g, b), tag="bank")
+                groups[g]["m2"].append(bank)
+                for cc in range(per_bank(g)):
+                    mx(bank[:, cc * n : (cc + 1) * n], "w2", per_bank(g) * b + cc, g, "r", 0, n, True, True)
 
-        def sub(g, b):
+        def sub(g):
             if not ok(g):
                 return
             st = groups[g]
-            if b == 0:
-                st["dy"] = work.tile([P, 4, GROUP], F32, name="dy%d" % g, tag="dy", bufs=4)
-            bank = st["m2_%d" % b]
-            for cc in range(2):
-                c = 2 * b + cc
+            n = width(g)
+            if not off(g):
+                st["dy"] = work.tile([P, 4, 256], F32, name="dy%d" % g, tag="dy", bufs=5)
+            for c in range(4):
+                if c in off(g):
+                    continue
+                b, cc = c // per_bank(g), c % per_bank(g)
                 nc.vector.scalar_tensor_tensor(
-                    out=st["dy"][:, c, :],
-                    in0=bank[:, cc * GROUP : (cc + 1) * GROUP],
+                    out=st["dy"][:, c, 0:n],
+                    in0=st["m2"][b][:, cc * n : (cc + 1) * n],
                     scalar=bias[:, 4 + c : 5 + c],
                     in1=grouped(g, "x").rearrange("p (n t) -> p n t", t=4)[:, :, c],
                     op0=ALU.add,
                     op1=ALU.subtract,
                 )
 
-        def cm(g, jj):
-            if not ok(g):
+        def off(g):
+            return []
+
+        def sub_s(g):
+            if not ok(g) or not off(g):
+                return
+            st = groups[g]
+            n = width(g)
+            st["dy"] = work.tile([P, 4, 256], F32, name="dy%d" % g, tag="dy", bufs=5)
+            for c in off(g):
+                b, cc = c // per_bank(g), c % per_bank(g)
+                nc.scalar.activation(
+                    out=st["dy"][:, c, 0:n], in_=st["m2"][b][:, cc * n : (cc + 1) * n], func=ACT.Identity, bias=bias[:, 4 + c : 5 + c], scale=1.0
+                )
+                nc.gpsimd.tensor_tensor(
+                    out=st["dy"][:, c, 0:n], in0=st["dy"][:, c, 0:n], in1=grouped(g, "x").rearrange("p (n t) -> p n t", t=4)[:, :, c], op=ALU.subtract
+                )
+
+        def cm(g, jj, on_vector=False):
+            if not ok(g) or jj >= plan[g][2]:
                 return
             st = groups[g]
             tok = slice(jj * P, (jj + 1) * P)
-            nc.gpsimd.tensor_tensor(out=st["dy"][:, :, tok], in0=st["dy"][:, :, tok], in1=st["h"][:, :, tok], op=ALU.mult)
+            eng = nc.vector if on_vector else nc.gpsimd
+            eng.tensor_tensor(out=st["dy"][:, :, tok], in0=st["dy"][:, :, tok], in1=st["h"][:, :, tok], op=ALU.mult)
 
         def tbx(g, jj):
-            if not ok(g):
+            if not ok(g) or jj >= plan[g][2]:
                 return
             st = groups[g]
+            s, j0, nj = plan[g]
             if jj == 0:
                 st["yc"] = work.tile([P, 2, WIDTH], F32, name="yc%d" % g, tag="yc")
                 for key in ("sums", "nmu", "ssq"):
                     st[key] = stat.tile([P, 2], F32, name="%s%d" % (key, g), tag=key)
-            bank = banks.tile([P, 512], F32, name="tb%d_%d" % (g, jj), tag="bank")
-            st["tb%d" % jj] = bank
-            nc.tensor.matmul(
-                out=bank[:],
-                lhsT=identb[:],
-                rhs=supers[g // 2]["x"][:, 2 * (g % 2) + jj, :],
-                start=True,
-                stop=False,
-            )
+            st["tb%d" % jj] = banks.tile([P, 512], F32, name="tb%d_%d" % (g, jj), tag="bank")
+            nc.tensor.matmul(out=st["tb%d" % jj][:], lhsT=identb[:], rhs=supers[s]["x"][:, j0 + jj, :], start=True, stop=False)
+
         def tbt(g, jj, c):
-            if ok(g):
-                st = groups[g]
-                bank = st["tb%d" % jj]
-                nc.tensor.matmul(
-                    out=bank[:].rearrange("p (m t) -> p m t", t=4)[:, :, c],
-                    lhsT=st["dy"][:, c, jj * P : (jj + 1) * P],
-                    rhs=identf[:],
-                    is_transpose=True,
-                    start=False,
-                    stop=(c == 3),
-                )
+            if not ok(g) or jj >= plan[g][2]:
+                return
+            st = groups[g]
+            nc.tensor.matmul(
+                out=st["tb%d" % jj][:].rearrange("p (m t) -> p m t", t=4)[:, :, c],
+                lhsT=st["dy"][:, c, jj * P : (jj + 1) * P],
+                rhs=identf[:],
+                is_transpose=True,
+                start=False,
+                stop=(c == 3),
+            )
+
         def tbo(g, jj):
-            if not ok(g):
+            if not ok(g) or jj >= plan[g][2]:
                 return
             st = groups[g]
             nc.scalar.activation(
-                out=st["yc"][:, jj, :],
-                in_=st["tb%d" % jj][:],
-                func=ACT.Identity,
-                accum_out=st["sums"][:, jj : jj + 1],
+                out=st["yc"][:, jj, :], in_=st["tb%d" % jj][:], func=ACT.Identity, accum_out=st["sums"][:, jj : jj + 1]
             )
 
         def tb(g, jj):
@@ -326,111 +389,104 @@ def tile_rotelearningmemory_pa_t_kernel(
                 tbt(g, jj, c)
             tbo(g, jj)
 
-        def mean(g, jj):
-            if not ok(g):
-                return
-            st = groups[g]
-            one = slice(jj, jj + 1)
-            nc.scalar.mul(out=st["nmu"][:, one], in_=st["sums"][:, one], mul=-1.0 / WIDTH)
+        def mean(g):
+            if ok(g):
+                st = groups[g]
+                n = plan[g][2]
+                nc.scalar.mul(out=st["nmu"][:, 0:n], in_=st["sums"][:, 0:n], mul=-1.0 / WIDTH)
 
-        def s2(g, jj):
+        def s2(g):
             if not ok(g):
                 return
             st = groups[g]
-            one = slice(jj, jj + 1)
-            nc.scalar.activation(
-                out=junk[:], in_=st["yc"][:, jj, :], func=ACT.Square, bias=st["nmu"][:, one], scale=1.0,
-                accum_out=st["ssq"][:, one],
-            )
+            for jj in range(plan[g][2]):
+                one = slice(jj, jj + 1)
+                nc.scalar.activation(
+                    out=junk[jj][:], in_=st["yc"][:, jj, :], func=ACT.Square, bias=st["nmu"][:, one], scale=1.0, accum_out=st["ssq"][:, one]
+                )
 
         def pw(g):
             if not ok(g):
                 return
             st = groups[g]
+            n = plan[g][2]
             st["var"] = stat.tile([P, 2], F32, name="var%d" % g, tag="var")
             st["rs"] = stat.tile([P, 2], F32, name="rs%d" % g, tag="rs")
             nc.gpsimd.tensor_scalar(
-                out=st["var"][:], in0=st["ssq"][:], scalar1=1.0 / WIDTH, scalar2=LN_EPS, op0=ALU.mult, op1=ALU.add
+                out=st["var"][:, 0:n], in0=st["ssq"][:, 0:n], scalar1=1.0 / WIDTH, scalar2=LN_EPS, op0=ALU.mult, op1=ALU.add
             )
-            nc.gpsimd.tensor_tensor(out=st["rs"][:], in0=st["var"][:], in1=mhalf[:], op=ALU.pow)
+            nc.gpsimd.tensor_tensor(out=st["rs"][:, 0:n], in0=st["var"][:, 0:n], in1=mhalf[:, 0:n], op=ALU.pow)
 
-        def ln1(g, jj):
+        def ln1(g):
             if not ok(g):
                 return
             st = groups[g]
-            if jj == 0:
-                st["o"] = work.tile([P, 2, WIDTH], F32, name="o%d" % g, tag="o")
-            nc.vector.scalar_tensor_tensor(
-                out=st["o"][:, jj, :], in0=st["yc"][:, jj, :], scalar=st["nmu"][:, jj : jj + 1], in1=lnbank[:, 0:WIDTH],
-                op0=ALU.add, op1=ALU.mult,
-            )
-
-        def ln2(g, jj):
-            if not ok(g):
-                return
-            st = groups[g]
-            nc.vector.scalar_tensor_tensor(
-                out=st["o"][:, jj, :], in0=st["o"][:, jj, :], scalar=st["rs"][:, jj : jj + 1],
-                in1=lnbank[:, WIDTH : 2 * WIDTH], op0=ALU.mult, op1=ALU.add,
-            )
-            if jj == 1:
-                s = g // 2
-                first = 2 * (g % 2)
-                nc.sync.dma_start(
-                    out=o_rows[s * SUPER : (s + 1) * SUPER, :].rearrange("(p j) d -> p j d", j=4)[:, first : first + 2, :],
-                    in_=st["o"][:],
+            st["o"] = work.tile([P, 2, WIDTH], F32, name="o%d" % g, tag="o", bufs=4)
+            for jj in range(plan[g][2]):
+                nc.vector.scalar_tensor_tensor(
+                    out=st["o"][:, jj, :], in0=st["yc"][:, jj, :], scalar=st["nmu"][:, jj : jj + 1], in1=lnbank[:, 0:WIDTH],
+                    op0=ALU.add, op1=ALU.mult,
                 )
 
+        def ln2(g, split=False):
+            if not ok(g):
+                return
+            st = groups[g]
+            s, j0, nj = plan[g]
+            rows = o_rows[s * SUPER : (s + 1) * SUPER, :].rearrange("(p j) d -> p j d", j=4)
+            for jj in range(nj):
+                nc.vector.scalar_tensor_tensor(
+                    out=st["o"][:, jj, :], in0=st["o"][:, jj, :], scalar=st["rs"][:, jj : jj + 1],
+                    in1=lnbank[:, WIDTH : 2 * WIDTH], op0=ALU.mult, op1=ALU.add,
+                )
+                if split:
+                    nc.sync.dma_start(out=rows[:, j0 + jj : j0 + jj + 1, :], in_=st["o"][:, jj : jj + 1, :])
+            if not split:
+                nc.sync.dma_start(out=rows[:, j0 : j0 + nj, :], in_=st["o"][:, 0:nj, :])
+
+        alloc(0)
+        w1raw = load_weight(attn_out_w, 0, "w1raw")
+        fetch(0, "c", 0, 2)
+        fetch(0, "x", 0, 2)
+        fetch(0, "q", 0, 2)
+        wgxraw = load_weight(gate_w, 0, "wgxraw")
+        fetch(0, "c", 2, 2)
+        wgqraw = load_weight(gate_w, 512, "wgqraw")
+        w2raw = load_weight(op_w, 0, "w2raw")
+        fetch(0, "x", 2, 2)
+        fetch(0, "q", 2, 2)
         loaded = 1
-        for t in range(-3, N_GROUPS + 4):
-            while loaded < N_GROUPS // 2 and 2 * loaded - 6 <= t:
+        for t in range(-2, N_GROUPS + 4):
+            while loaded < N_SUPERS and 2 * loaded - 5 <= t:
                 load(loaded)
                 loaded += 1
-            if t == -3:
-                weights["w1"] = prepare_weight(w1raw, 0, "w1")
-            ln1(t - 4, 0)
-            ln1(t - 4, 1)
-            q_rc(t)
+            if t == -2:
+                prepare_weight(w1raw, "w1")
             q_xq(t + 1)
+            q_rc(t)
             if t == -1:
-                weights["wgx"] = prepare_weight(wgraw, 0, "wgx")
-                weights["wgq"] = prepare_weight(wgraw, 512, "wgq")
+                prepare_weight(wgxraw, "wgx")
+                prepare_weight(wgqraw, "wgq")
             if t == 0:
-                weights["w2"] = prepare_weight(w2raw, 0, "w2")
+                prepare_weight(w2raw, "w2")
             if t == 1:
-                nc.tensor.matmul(out=lnbank[:, 0:WIDTH], lhsT=ones[:], rhs=lnrow[:, 0:WIDTH], start=True, stop=True)
-                nc.tensor.matmul(
-                    out=lnbank[:, WIDTH : 2 * WIDTH], lhsT=ones[:], rhs=lnrow[:, WIDTH : 2 * WIDTH], start=True, stop=True
-                )
-            ti(t + 3, "c")
-            tbx(t - 3, 1)
-            ti_open(t + 2, "x")
-            for i in range(4):
-                tbt(t - 3, 1, i)
-                ti_t(t + 2, "x", i)
-            tbo(t - 3, 1)
-            mean(t - 3, 0)
-            ti_out(t + 2, "x")
-            mean(t - 3, 1)
-            s2(t - 3, 0)
-            s2(t - 3, 1)
+                spread_ln()
+            tb(t - 3, 1)
+            ti(t + 2, "c")
+            mean(t - 3)
+            ti(t + 2, "x")
+            s2(t - 3)
             pw(t - 3)
-            m2(t - 1, 0)
-            m2(t - 1, 1)
-            m3(t, 0)
-            m3(t, 1)
-            sub(t - 1, 0)
-            sub(t - 1, 1)
+            m2(t - 1)
+            m3(t)
+            sg(t)
+            sub(t - 1)
             cm(t - 1, 0)
             cm(t - 1, 1)
-            ln2(t - 4, 0)
-            ln2(t - 4, 1)
-            tbx(t - 2, 0)
-            ti_open(t + 2, "q")
-            for i in range(4):
-                tbt(t - 2, 0, i)
-                ti_t(t + 2, "q", i)
-            tbo(t - 2, 0)
-            ti_out(t + 2, "q")
-            m1(t + 1, 0)
-            m1(t + 1, 1)
+            ln1(t - 3)
+            ln2(t - 4, t - 4 == N_GROUPS - 1)
+            tb(t - 2, 0)
+            ti(t + 2, "q")
+            if t == -2:
+                prepare_bias()
+            m1(t + 1)

@@ -55,15 +55,23 @@ def tile_rotelearningmemory_pa_t_kernel(
         btile = const.tile([P, WIDTH], BF16, name="btile")
         nc.vector.memset(btile[:], 0.0)
         junk = [const.tile([P, WIDTH], BF16, name="junk%d" % i) for i in range(2)]
-        for v, vec in enumerate((attn_out_b, op_b, gate_b)):
-            nc.scalar.dma_start(out=btile[v : v + 1, :], in_=vec.rearrange("(o w) -> o w", o=1))
+
+        def load_bias():
+            for v, vec in enumerate((attn_out_b, op_b, gate_b)):
+                nc.sync.dma_start(out=btile[v : v + 1, :], in_=vec.rearrange("(o w) -> o w", o=1))
+
+        def load_ln():
+            nc.sync.dma_start(out=lnrow[0:1, 0:WIDTH], in_=ln_g.rearrange("(o d) -> o d", o=1))
+            nc.sync.dma_start(out=lnrow[0:1, WIDTH : 2 * WIDTH], in_=ln_b.rearrange("(o d) -> o d", o=1))
+
         lnrow = const.tile([P, 2 * WIDTH], BF16, name="lnrow")
         nc.vector.memset(lnrow[:], 0.0)
-        nc.scalar.dma_start(out=lnrow[0:1, 0:WIDTH], in_=ln_g.rearrange("(o d) -> o d", o=1))
-        nc.scalar.dma_start(out=lnrow[0:1, WIDTH : 2 * WIDTH], in_=ln_b.rearrange("(o d) -> o d", o=1))
         ones = const.tile([P, P], BF16, name="ones")
         nc.vector.memset(ones[:], 1.0)
         lnbank = pc.tile([P, 2 * WIDTH], BF16, name="lnbank")
+
+        first_act = const.tile([P, 1], F32, name="first_act")
+        nc.scalar.activation(out=first_act[:], in_=mhalf[:, 0:1], func=ACT.Sigmoid)
 
         supers = {}
 
@@ -449,10 +457,12 @@ def tile_rotelearningmemory_pa_t_kernel(
         fetch(0, "c", 0, 2)
         fetch(0, "x", 0, 2)
         fetch(0, "q", 0, 2)
+        load_bias()
         wgxraw = load_weight(gate_w, 0, "wgxraw")
         fetch(0, "c", 2, 2)
         wgqraw = load_weight(gate_w, 512, "wgqraw")
         w2raw = load_weight(op_w, 0, "w2raw")
+        load_ln()
         fetch(0, "x", 2, 2)
         fetch(0, "q", 2, 2)
         loaded = 1
@@ -475,6 +485,8 @@ def tile_rotelearningmemory_pa_t_kernel(
             ti(t + 2, "c")
             mean(t - 3)
             ti(t + 2, "x")
+            if t < 2:
+                ti(t + 2, "q")
             s2(t - 3)
             pw(t - 3)
             m2(t - 1)
@@ -486,7 +498,8 @@ def tile_rotelearningmemory_pa_t_kernel(
             ln1(t - 3)
             ln2(t - 4, t - 4 == N_GROUPS - 1)
             tb(t - 2, 0)
-            ti(t + 2, "q")
+            if t >= 2:
+                ti(t + 2, "q")
             if t == -2:
                 prepare_bias()
             m1(t + 1)

@@ -14,7 +14,11 @@ ACT = mybir.ActivationFunctionType
 P = 128
 TOKENS = 4096
 WIDTH = 512
-SUPER = 512
+SLOTS = 4
+CHUNKS = WIDTH // P
+GROUP = 2 * P
+SUPER = 4 * P
+N_GROUPS = TOKENS // GROUP
 N_SUPERS = TOKENS // SUPER
 LN_EPS = 1e-5
 FLOPS = 2 * TOKENS * WIDTH * (512 + 512 + 1024)
@@ -25,14 +29,7 @@ def tile_rotelearningmemory_pa_t_kernel(
 ):
     nc = tc.nc
     sources = {"x": x.flatten_outer_dims(), "q": query.flatten_outer_dims(), "c": ctx.flatten_outer_dims()}
-    o_rows = out.flatten_outer_dims()
-
-    sizes = [2] * 16
-    plan = []
-    for n in sizes:
-        done = sum(p[2] for p in plan)
-        plan.append((done // 4, done % 4, n))
-    N_GROUPS = len(plan)
+    out_rows = out.flatten_outer_dims()
 
     with ExitStack() as stack:
         stack.enter_context(tc.manual_schedule())
@@ -43,103 +40,107 @@ def tile_rotelearningmemory_pa_t_kernel(
         cods = stack.enter_context(tc.tile_pool(name="cods", bufs=3))
         work = stack.enter_context(tc.tile_pool(name="work", bufs=3))
         stat = stack.enter_context(tc.tile_pool(name="stat", bufs=4))
-        pc = stack.enter_context(tc.psum_pool(name="pc", bufs=1))
+        ln_pool = stack.enter_context(tc.psum_pool(name="ln_pool", bufs=1))
         banks = stack.enter_context(tc.psum_pool(name="banks", bufs=7))
 
         identf = const.tile([P, P], F32, name="identf")
         make_identity(nc, identf[:])
         identb = const.tile([P, P], BF16, name="identb")
         make_identity(nc, identb[:])
-        mhalf = const.tile([P, 2], F32, name="mhalf")
-        nc.gpsimd.memset(mhalf[:], -0.5)
-        btile = const.tile([P, WIDTH], BF16, name="btile")
-        nc.vector.memset(btile[:], 0.0)
-        junk = [const.tile([P, WIDTH], BF16, name="junk%d" % i) for i in range(2)]
+        minus_half = const.tile([P, 2], F32, name="minus_half")
+        nc.gpsimd.memset(minus_half[:], -0.5)
+        first_act = const.tile([P, 1], F32, name="first_act")
+        nc.scalar.activation(out=first_act[:], in_=minus_half[:, 0:1], func=ACT.Sigmoid)
+        squares = [const.tile([P, WIDTH], BF16, name="squares%d" % jj) for jj in range(2)]
 
-        def load_bias():
-            for v, vec in enumerate((attn_out_b, op_b, gate_b)):
-                nc.sync.dma_start(out=btile[v : v + 1, :], in_=vec.rearrange("(o w) -> o w", o=1))
-
-        def load_ln():
-            nc.sync.dma_start(out=lnrow[0:1, 0:WIDTH], in_=ln_g.rearrange("(o d) -> o d", o=1))
-            nc.sync.dma_start(out=lnrow[0:1, WIDTH : 2 * WIDTH], in_=ln_b.rearrange("(o d) -> o d", o=1))
-
-        lnrow = const.tile([P, 2 * WIDTH], BF16, name="lnrow")
-        nc.vector.memset(lnrow[:], 0.0)
+        vectors = const.tile([P, WIDTH], BF16, name="vectors")
+        nc.vector.memset(vectors[:], 0.0)
+        ln_rows = const.tile([P, 2 * WIDTH], BF16, name="ln_rows")
+        nc.vector.memset(ln_rows[:], 0.0)
         ones = const.tile([P, P], BF16, name="ones")
         nc.vector.memset(ones[:], 1.0)
-        lnbank = pc.tile([P, 2 * WIDTH], BF16, name="lnbank")
-
-        first_act = const.tile([P, 1], F32, name="first_act")
-        nc.scalar.activation(out=first_act[:], in_=mhalf[:, 0:1], func=ACT.Sigmoid)
+        ln_bank = ln_pool.tile([P, 2 * WIDTH], BF16, name="ln_bank")
 
         supers = {}
 
-        def alloc(s):
+        def new_super(s):
             supers[s] = {}
             for key, bufs in (("c", 3), ("x", 6), ("q", 3)):
-                supers[s][key] = raws.tile([P, 4, WIDTH], BF16, name="raw%s%d" % (key, s), tag="raw" + key, bufs=bufs)
+                supers[s][key] = raws.tile([P, 4, WIDTH], BF16, name="%s%d" % (key, s), tag=key, bufs=bufs)
 
-        def fetch(s, key, j0, nj):
+        def fetch(s, key, first, count):
             rows = sources[key][s * SUPER : (s + 1) * SUPER, :].rearrange("(p j) k -> p j k", j=4)
-            nc.sync.dma_start(out=supers[s][key][:, j0 : j0 + nj, :], in_=rows[:, j0 : j0 + nj, :])
-
-        def load(s):
-            alloc(s)
-            for key in ("c", "x", "q"):
-                fetch(s, key, 0, 4)
+            part = slice(first, first + count)
+            nc.sync.dma_start(out=supers[s][key][:, part, :], in_=rows[:, part, :])
 
         def load_weight(w, k0, name):
-            raw = const.tile([P, 4, 512], BF16, name=name)
-            src = w.rearrange("(m t) k -> m t k", t=4)[:, :, k0 : k0 + 512]
-            nc.sync.dma_start(out=raw[:], in_=src)
+            raw = const.tile([P, SLOTS, WIDTH], BF16, name=name)
+            nc.sync.dma_start(out=raw[:], in_=w.rearrange("(m t) k -> m t k", t=SLOTS)[:, :, k0 : k0 + WIDTH])
             return raw
 
-        def transposes(bank, src, first, n):
-            for jj in range(n):
-                words = src[:, first + jj, :].bitcast(F32)
-                for u in range(2):
-                    col = u * n * P + jj * P
-                    nc.tensor.transpose(bank[:, col : col + P], words[:, u : 2 * P : 2], identf[:])
+        new_super(0)
+        w1_raw = load_weight(attn_out_w, 0, "w1_raw")
+        for key in ("c", "x", "q"):
+            fetch(0, key, 0, 2)
+        for row, vec in enumerate((attn_out_b, op_b, gate_b)):
+            nc.sync.dma_start(out=vectors[row : row + 1, :], in_=vec.rearrange("(o w) -> o w", o=1))
+        wgx_raw = load_weight(gate_w, 0, "wgx_raw")
+        fetch(0, "c", 2, 2)
+        wgq_raw = load_weight(gate_w, WIDTH, "wgq_raw")
+        w2_raw = load_weight(op_w, 0, "w2_raw")
+        for half, vec in enumerate((ln_g, ln_b)):
+            cols = slice(half * WIDTH, (half + 1) * WIDTH)
+            nc.sync.dma_start(out=ln_rows[0:1, cols], in_=vec.rearrange("(o d) -> o d", o=1))
+        fetch(0, "x", 2, 2)
+        fetch(0, "q", 2, 2)
 
-        def leave(on_vector, dst, bank):
-            if on_vector:
-                nc.vector.tensor_copy(out=dst, in_=bank)
-            else:
-                nc.scalar.copy(out=dst, in_=bank)
+        def transpose_words(bank, src, jj, u):
+            col = u * GROUP + jj * P
+            nc.tensor.transpose(bank[:, col : col + P], src.bitcast(F32)[:, u : 2 * P : 2], identf[:])
+
+        def as_words(dst):
+            return dst.bitcast(F32).rearrange("p (n u) -> p n u", u=2)
+
+        def interleaved(bank):
+            return bank[:].rearrange("p (u n) -> p n u", u=2)
+
+        weights = {}
 
         def prepare_weight(raw, name):
-            grp = wtmp.tile([P, 2048], BF16, name="g" + name, tag="wgrp", align_bytes=64)
-            words = grp[:].bitcast(F32).rearrange("p (n u) -> p n u", u=2)
+            grp = wtmp.tile([P, SLOTS * WIDTH], BF16, name="grp_" + name, tag="wgrp", align_bytes=64)
             for half in range(2):
-                bank = banks.tile([P, 512], F32, name="b%s%d" % (name, half), tag="bank")
-                transposes(bank, raw, 2 * half, 2)
-                leave(half == 1, words[:, half * 256 : (half + 1) * 256, :], bank[:].rearrange("p (u n) -> p n u", u=2))
-            codes = const.tile([P, 512], U32, name="c" + name, align_bytes=64)
-            scales = const.tile([P, 512], U8, name="s" + name, align_bytes=64)
+                bank = banks.tile([P, 512], F32, name="%s_%d" % (name, half), tag="bank")
+                for jj in range(2):
+                    for u in range(2):
+                        transpose_words(bank, raw[:, 2 * half + jj, :], jj, u)
+                cols = slice(half * SLOTS * GROUP, (half + 1) * SLOTS * GROUP)
+                if half == 0:
+                    nc.scalar.copy(out=as_words(grp[:, cols]), in_=interleaved(bank))
+                else:
+                    nc.vector.tensor_copy(out=as_words(grp[:, cols]), in_=interleaved(bank))
+            codes = const.tile([P, WIDTH], U32, name="codes_" + name, align_bytes=64)
+            scales = const.tile([P, WIDTH], U8, name="scales_" + name, align_bytes=64)
             nc.vector.quantize_mx(out=codes[:].bitcast(FP8X4), scales=scales[:], in_=grp[:])
             weights[name] = (codes, scales)
 
-        weights = {}
-        bias = const.tile([P, 12], F32, name="bias")
-        nbg = const.tile([P, 4], F32, name="nbg")
+        bias = const.tile([P, 3 * CHUNKS], F32, name="bias")
+        minus_gate_bias = const.tile([P, CHUNKS], F32, name="minus_gate_bias")
 
         def prepare_bias():
-            bbank = banks.tile([P, 512], F32, name="bbank", tag="bank")
+            bank = banks.tile([P, 512], F32, name="bias_bank", tag="bank")
             for u in range(2):
-                nc.tensor.transpose(bbank[:, u * P : (u + 1) * P], btile[:].bitcast(F32)[:, u : 2 * P : 2], identf[:])
-            bwords = const.tile([P, 8], F32, name="bwords")
-            nc.vector.tensor_copy(
-                out=bwords[:, 0:6].rearrange("p (v u) -> p v u", u=2),
-                in_=bbank[:, 0 : 2 * P].rearrange("p (u v) -> p v u", u=2)[:, 0:3, :],
+                transpose_words(bank, vectors[:], 0, u)
+            words = const.tile([P, 8], F32, name="bias_words")
+            nc.vector.tensor_copy(out=as_words(words[:, 0:6]), in_=interleaved(bank)[:, 0:3, :])
+            nc.vector.tensor_copy(out=bias[:], in_=words[:, 0:6].bitcast(BF16))
+            nc.vector.tensor_scalar(
+                out=minus_gate_bias[:], in0=bias[:, 8:12], scalar1=-1.0, scalar2=None, op0=ALU.mult
             )
-            nc.vector.tensor_copy(out=bias[:], in_=bwords[:, 0:6].bitcast(BF16))
-            nc.vector.tensor_scalar(out=nbg[:], in0=bias[:, 8:12], scalar1=-1.0, scalar2=None, op0=ALU.mult)
 
         def spread_ln():
-            for h in range(2):
-                cols = slice(h * WIDTH, (h + 1) * WIDTH)
-                nc.tensor.matmul(out=lnbank[:, cols], lhsT=ones[:], rhs=lnrow[:, cols], start=True, stop=True)
+            for half in range(2):
+                cols = slice(half * WIDTH, (half + 1) * WIDTH)
+                nc.tensor.matmul(out=ln_bank[:, cols], lhsT=ones[:], rhs=ln_rows[:, cols], start=True, stop=True)
 
         groups = [{} for g in range(N_GROUPS)]
         pairs = {}
@@ -147,359 +148,253 @@ def tile_rotelearningmemory_pa_t_kernel(
         def ok(g):
             return 0 <= g < N_GROUPS
 
-        def home(g, key):
-            if key in ("r", "c"):
-                name, bufs, half = ("rc", g if key == "r" else g - 1), 3, (0 if key == "r" else 1)
-            else:
-                name, bufs, half = ("xq", g), 5, (0 if key == "x" else 1)
+        def place(g, key):
+            name = {"r": ("rc", g), "c": ("rc", g - 1), "x": ("xq", g), "q": ("xq", g)}[key]
             if name not in pairs:
                 pairs[name] = {
-                    "grp": grps.tile([P, 8 * 256], BF16, name="g%s%d" % (name[0], name[1] + 4), tag="g" + name[0], bufs=bufs, align_bytes=64)
+                    "grp": grps.tile(
+                        [P, 2 * SLOTS * GROUP],
+                        BF16,
+                        name="grp_%s%d" % (name[0], name[1] + 1),
+                        tag=name[0],
+                        bufs=(3 if name[0] == "rc" else 5),
+                        align_bytes=64,
+                    )
                 }
-            return pairs[name], half
-
-        def width(g):
-            return plan[g][2] * P
-
-        def place(g, key):
-            pair, half = home(g, key)
-            if half == 0:
-                return pair, 0
-            mate = g if key == "q" else g - 1
-            return pair, (width(mate) if ok(mate) else 0)
+            return pairs[name], (0 if key in ("r", "x") else 1)
 
         def grouped(g, key):
-            pair, col = place(g, key)
-            return pair["grp"][:, 4 * col : 4 * (col + width(g))]
+            pair, half = place(g, key)
+            return pair["grp"][:, half * SLOTS * GROUP : (half + 1) * SLOTS * GROUP]
 
-        def quantise(name, cols):
+        def quantise(name, first, last):
             pair = pairs[name]
-            label = "%s%d" % (name[0], name[1] + 4)
-            if "codes" not in pair:
-                pair["codes"] = cods.tile([P, 512], U32, name="c" + label, tag="c" + name[0], align_bytes=64)
-                pair["scales"] = cods.tile([P, 512], U8, name="s" + label, tag="s" + name[0], align_bytes=64)
-            while cols[0] < cols[1]:
-                n = cols[1] - cols[0]
-                n = 512 if n >= 512 else (256 if n >= 256 else 128)
-                sl = slice(cols[0], cols[0] + n)
-                nc.vector.quantize_mx(
-                    out=pair["codes"][:, sl].bitcast(FP8X4),
-                    scales=pair["scales"][:, sl],
-                    in_=pair["grp"][:, 4 * cols[0] : 4 * (cols[0] + n)],
-                )
-                cols = (cols[0] + n, cols[1])
+            label = "%s%d" % (name[0], name[1] + 1)
+            pair["codes"] = cods.tile([P, 2 * GROUP], U32, name="codes_" + label, tag="codes_" + name[0], align_bytes=64)
+            pair["scales"] = cods.tile([P, 2 * GROUP], U8, name="scales_" + label, tag="scales_" + name[0], align_bytes=64)
+            cols = slice(first * GROUP, last * GROUP)
+            nc.vector.quantize_mx(
+                out=pair["codes"][:, cols].bitcast(FP8X4),
+                scales=pair["scales"][:, cols],
+                in_=pair["grp"][:, first * SLOTS * GROUP : last * SLOTS * GROUP],
+            )
 
-        def q_one(g, key):
+        def quantise_rc(g):
+            first = 0 if ok(g) else 1
+            last = 2 if ok(g + 1) else 1
+            if first < last:
+                quantise(("rc", g), first, last)
+
+        def quantise_xq(g):
             if ok(g):
-                pair, col = place(g, key)
-                quantise(home_name(g, key), (col, col + width(g)))
+                quantise(("xq", g), 0, 2)
 
-        def home_name(g, key):
-            return ("rc", g if key == "r" else g - 1) if key in ("r", "c") else ("xq", g)
+        def turn(g, key):
+            if not ok(g):
+                return
+            bank = banks.tile([P, 512], F32, name="turn_%s%d" % (key, g), tag="bank")
+            for jj in range(2):
+                for u in range(2):
+                    transpose_words(bank, supers[g // 2][key][:, 2 * (g % 2) + jj, :], jj, u)
+            nc.scalar.copy(out=as_words(grouped(g, key)), in_=interleaved(bank))
 
-        def q_rc(t):
-            first = 0 if ok(t) else None
-            c = t + 1
-            if ok(t) and ok(c):
-                quantise(("rc", t), (0, width(t) + width(c)))
-            elif ok(t):
-                q_one(t, "r")
-            elif ok(c):
-                q_one(c, "c")
-
-        def q_xq(g):
-            if ok(g):
-                quantise(("xq", g), (0, 2 * width(g)))
-
-        def ti_open(g, key):
-            if ok(g):
-                groups[g]["ti" + key] = banks.tile([P, 512], F32, name="ti%s%d" % (key, g), tag="bank")
-
-        def ti_n(g):
-            return 2 * plan[g][2] if ok(g) else 0
-
-        def ti_t(g, key, i):
-            if ok(g) and i < ti_n(g):
-                s, j0, nj = plan[g]
-                jj, u = i // 2, i % 2
-                words = supers[s][key][:, j0 + jj, :].bitcast(F32)
-                col = u * nj * P + jj * P
-                nc.tensor.transpose(groups[g]["ti" + key][:, col : col + P], words[:, u : 2 * P : 2], identf[:])
-
-        def ti_out(g, key, on_vector=False):
-            if ok(g):
-                n = width(g)
-                leave(
-                    on_vector,
-                    grouped(g, key).bitcast(F32).rearrange("p (n u) -> p n u", u=2),
-                    groups[g]["ti" + key][:, 0 : 2 * n].rearrange("p (u n) -> p n u", u=2),
-                )
-
-        def ti(g, key, on_vector=False):
-            ti_open(g, key)
-            for i in range(4):
-                ti_t(g, key, i)
-            ti_out(g, key, on_vector)
-
-        def mx(dst, wkey, c, g, key, first, count, start, stop):
-            wc, ws = weights[wkey]
-            pair, at = place(g, key)
-            col = slice(c * P, (c + 1) * P)
-            cols = slice(at + first, at + first + count)
+        def mx(dst, weight, c, g, key, first, count, start, stop):
+            codes, scales = weights[weight]
+            pair, half = place(g, key)
+            channels = slice(c * P, (c + 1) * P)
+            tokens = slice(half * GROUP + first, half * GROUP + first + count)
             nc.tensor.matmul_mx(
                 out=dst,
-                lhsT=wc[:, col].bitcast(FP8X4),
-                lhsT_scale=ws[:, col],
-                rhs=pair["codes"][:, cols].bitcast(FP8X4),
-                rhs_scale=pair["scales"][:, cols],
+                lhsT=codes[:, channels].bitcast(FP8X4),
+                lhsT_scale=scales[:, channels],
+                rhs=pair["codes"][:, tokens].bitcast(FP8X4),
+                rhs_scale=pair["scales"][:, tokens],
                 start=start,
                 stop=stop,
             )
 
-        def m1(g):
+        def product_r(g):
             if not ok(g):
                 return
-            for jj in range(plan[g][2]):
-                bank = banks.tile([P, 512], F32, name="m1_%d_%d" % (g, jj), tag="bank")
-                for c in range(4):
+            for jj in range(2):
+                bank = banks.tile([P, 512], F32, name="r%d_%d" % (g, jj), tag="bank")
+                for c in range(CHUNKS):
                     mx(bank[:, c * P : (c + 1) * P], "w1", c, g, "c", jj * P, P, True, True)
                 nc.vector.tensor_tensor(
-                    out=grouped(g, "r").rearrange("p (n c) -> p n c", c=4)[:, jj * P : (jj + 1) * P, :],
-                    in0=bank[:].rearrange("p (c n) -> p n c", c=4),
-                    in1=bias[:, 0:4].unsqueeze(1).to_broadcast([P, P, 4]),
+                    out=grouped(g, "r").rearrange("p (n c) -> p n c", c=CHUNKS)[:, jj * P : (jj + 1) * P, :],
+                    in0=bank[:].rearrange("p (c n) -> p n c", c=CHUNKS),
+                    in1=bias[:, 0:4].unsqueeze(1).to_broadcast([P, P, CHUNKS]),
                     op=ALU.add,
                 )
 
-        def per_bank(g):
-            return 512 // width(g)
+        def chunk_of(two_banks, c):
+            return two_banks[c // 2][:, (c % 2) * GROUP : (c % 2 + 1) * GROUP]
 
-        def m3(g):
+        def product_ret(g):
+            if not ok(g):
+                return
+            groups[g]["ret"] = [banks.tile([P, 512], F32, name="ret%d_%d" % (g, b), tag="bank") for b in range(2)]
+            for c in range(CHUNKS):
+                mx(chunk_of(groups[g]["ret"], c), "w2", c, g, "r", 0, GROUP, True, True)
+
+        def product_gate(g):
             if not ok(g):
                 return
             st = groups[g]
-            n = width(g)
-            st["h"] = work.tile([P, 4, 256], F32, name="h%d" % g, tag="h", bufs=5)
-            st["m3"] = []
-            for b in range(4 // per_bank(g)):
-                bank = banks.tile([P, 512], F32, name="m3_%d_%d" % (g, b), tag="bank")
-                st["m3"].append(bank)
-                for cc in range(per_bank(g)):
-                    part = bank[:, cc * n : (cc + 1) * n]
-                    c = per_bank(g) * b + cc
-                    mx(part, "wgx", c, g, "x", 0, n, True, False)
-                    mx(part, "wgq", c, g, "q", 0, n, False, True)
-
-        def sg(g):
-            if not ok(g):
-                return
-            st = groups[g]
-            n = width(g)
-            for c in range(4):
-                b, cc = c // per_bank(g), c % per_bank(g)
+            st["h"] = work.tile([P, CHUNKS, GROUP], F32, name="h%d" % g, tag="h", bufs=4)
+            gate = [banks.tile([P, 512], F32, name="gate%d_%d" % (g, b), tag="bank") for b in range(2)]
+            for c in range(CHUNKS):
+                mx(chunk_of(gate, c), "wgx", c, g, "x", 0, GROUP, True, False)
+                mx(chunk_of(gate, c), "wgq", c, g, "q", 0, GROUP, False, True)
+            for c in range(CHUNKS):
                 nc.scalar.activation(
-                    out=st["h"][:, c, 0:n], in_=st["m3"][b][:, cc * n : (cc + 1) * n], func=ACT.Sigmoid,
-                    bias=nbg[:, c : c + 1], scale=-1.0,
+                    out=st["h"][:, c, :],
+                    in_=chunk_of(gate, c),
+                    func=ACT.Sigmoid,
+                    bias=minus_gate_bias[:, c : c + 1],
+                    scale=-1.0,
                 )
 
-        def m2(g):
-            if not ok(g):
-                return
-            n = width(g)
-            groups[g]["m2"] = []
-            for b in range(4 // per_bank(g)):
-                bank = banks.tile([P, 512], F32, name="m2_%d_%d" % (g, b), tag="bank")
-                groups[g]["m2"].append(bank)
-                for cc in range(per_bank(g)):
-                    mx(bank[:, cc * n : (cc + 1) * n], "w2", per_bank(g) * b + cc, g, "r", 0, n, True, True)
-
-        def sub(g):
+        def subtract(g):
             if not ok(g):
                 return
             st = groups[g]
-            n = width(g)
-            if not off(g):
-                st["dy"] = work.tile([P, 4, 256], F32, name="dy%d" % g, tag="dy", bufs=5)
-            for c in range(4):
-                if c in off(g):
-                    continue
-                b, cc = c // per_bank(g), c % per_bank(g)
+            st["d"] = work.tile([P, CHUNKS, GROUP], F32, name="d%d" % g, tag="d", bufs=5)
+            for c in range(CHUNKS):
                 nc.vector.scalar_tensor_tensor(
-                    out=st["dy"][:, c, 0:n],
-                    in0=st["m2"][b][:, cc * n : (cc + 1) * n],
+                    out=st["d"][:, c, :],
+                    in0=chunk_of(st["ret"], c),
                     scalar=bias[:, 4 + c : 5 + c],
-                    in1=grouped(g, "x").rearrange("p (n t) -> p n t", t=4)[:, :, c],
+                    in1=grouped(g, "x").rearrange("p (n t) -> p n t", t=SLOTS)[:, :, c],
                     op0=ALU.add,
                     op1=ALU.subtract,
                 )
 
-        def off(g):
-            return []
-
-        def sub_s(g):
-            if not ok(g) or not off(g):
+        def multiply(g):
+            if not ok(g):
                 return
             st = groups[g]
-            n = width(g)
-            st["dy"] = work.tile([P, 4, 256], F32, name="dy%d" % g, tag="dy", bufs=5)
-            for c in off(g):
-                b, cc = c // per_bank(g), c % per_bank(g)
-                nc.scalar.activation(
-                    out=st["dy"][:, c, 0:n], in_=st["m2"][b][:, cc * n : (cc + 1) * n], func=ACT.Identity, bias=bias[:, 4 + c : 5 + c], scale=1.0
-                )
+            for jj in range(2):
+                tile = slice(jj * P, (jj + 1) * P)
                 nc.gpsimd.tensor_tensor(
-                    out=st["dy"][:, c, 0:n], in0=st["dy"][:, c, 0:n], in1=grouped(g, "x").rearrange("p (n t) -> p n t", t=4)[:, :, c], op=ALU.subtract
+                    out=st["d"][:, :, tile], in0=st["d"][:, :, tile], in1=st["h"][:, :, tile], op=ALU.mult
                 )
 
-        def cm(g, jj, on_vector=False):
-            if not ok(g) or jj >= plan[g][2]:
+        def blend(g, jj):
+            if not ok(g):
                 return
             st = groups[g]
-            tok = slice(jj * P, (jj + 1) * P)
-            eng = nc.vector if on_vector else nc.gpsimd
-            eng.tensor_tensor(out=st["dy"][:, :, tok], in0=st["dy"][:, :, tok], in1=st["h"][:, :, tok], op=ALU.mult)
-
-        def tbx(g, jj):
-            if not ok(g) or jj >= plan[g][2]:
-                return
-            st = groups[g]
-            s, j0, nj = plan[g]
             if jj == 0:
-                st["yc"] = work.tile([P, 2, WIDTH], F32, name="yc%d" % g, tag="yc")
-                for key in ("sums", "nmu", "ssq"):
+                st["y"] = work.tile([P, 2, WIDTH], F32, name="y%d" % g, tag="y")
+                for key in ("sum", "minus_mean", "sum_squares"):
                     st[key] = stat.tile([P, 2], F32, name="%s%d" % (key, g), tag=key)
-            st["tb%d" % jj] = banks.tile([P, 512], F32, name="tb%d_%d" % (g, jj), tag="bank")
-            nc.tensor.matmul(out=st["tb%d" % jj][:], lhsT=identb[:], rhs=supers[s]["x"][:, j0 + jj, :], start=True, stop=False)
-
-        def tbt(g, jj, c):
-            if not ok(g) or jj >= plan[g][2]:
-                return
-            st = groups[g]
+            bank = banks.tile([P, 512], F32, name="y%d_%d" % (g, jj), tag="bank")
             nc.tensor.matmul(
-                out=st["tb%d" % jj][:].rearrange("p (m t) -> p m t", t=4)[:, :, c],
-                lhsT=st["dy"][:, c, jj * P : (jj + 1) * P],
-                rhs=identf[:],
-                is_transpose=True,
-                start=False,
-                stop=(c == 3),
+                out=bank[:], lhsT=identb[:], rhs=supers[g // 2]["x"][:, 2 * (g % 2) + jj, :], start=True, stop=False
             )
-
-        def tbo(g, jj):
-            if not ok(g) or jj >= plan[g][2]:
-                return
-            st = groups[g]
+            for c in range(CHUNKS):
+                nc.tensor.matmul(
+                    out=bank[:].rearrange("p (m t) -> p m t", t=SLOTS)[:, :, c],
+                    lhsT=st["d"][:, c, jj * P : (jj + 1) * P],
+                    rhs=identf[:],
+                    is_transpose=True,
+                    start=False,
+                    stop=(c == CHUNKS - 1),
+                )
             nc.scalar.activation(
-                out=st["yc"][:, jj, :], in_=st["tb%d" % jj][:], func=ACT.Identity, accum_out=st["sums"][:, jj : jj + 1]
+                out=st["y"][:, jj, :], in_=bank[:], func=ACT.Identity, accum_out=st["sum"][:, jj : jj + 1]
             )
-
-        def tb(g, jj):
-            tbx(g, jj)
-            for c in range(4):
-                tbt(g, jj, c)
-            tbo(g, jj)
 
         def mean(g):
             if ok(g):
-                st = groups[g]
-                n = plan[g][2]
-                nc.scalar.mul(out=st["nmu"][:, 0:n], in_=st["sums"][:, 0:n], mul=-1.0 / WIDTH)
+                nc.scalar.mul(out=groups[g]["minus_mean"][:], in_=groups[g]["sum"][:], mul=-1.0 / WIDTH)
 
-        def s2(g):
+        def deviation(g):
             if not ok(g):
                 return
             st = groups[g]
-            for jj in range(plan[g][2]):
-                one = slice(jj, jj + 1)
+            for jj in range(2):
                 nc.scalar.activation(
-                    out=junk[jj][:], in_=st["yc"][:, jj, :], func=ACT.Square, bias=st["nmu"][:, one], scale=1.0, accum_out=st["ssq"][:, one]
+                    out=squares[jj][:],
+                    in_=st["y"][:, jj, :],
+                    func=ACT.Square,
+                    bias=st["minus_mean"][:, jj : jj + 1],
+                    scale=1.0,
+                    accum_out=st["sum_squares"][:, jj : jj + 1],
                 )
-
-        def pw(g):
-            if not ok(g):
-                return
-            st = groups[g]
-            n = plan[g][2]
-            st["var"] = stat.tile([P, 2], F32, name="var%d" % g, tag="var")
-            st["rs"] = stat.tile([P, 2], F32, name="rs%d" % g, tag="rs")
+            var = stat.tile([P, 2], F32, name="var%d" % g, tag="var")
+            st["rstd"] = stat.tile([P, 2], F32, name="rstd%d" % g, tag="rstd")
             nc.gpsimd.tensor_scalar(
-                out=st["var"][:, 0:n], in0=st["ssq"][:, 0:n], scalar1=1.0 / WIDTH, scalar2=LN_EPS, op0=ALU.mult, op1=ALU.add
+                out=var[:], in0=st["sum_squares"][:], scalar1=1.0 / WIDTH, scalar2=LN_EPS, op0=ALU.mult, op1=ALU.add
             )
-            nc.gpsimd.tensor_tensor(out=st["rs"][:, 0:n], in0=st["var"][:, 0:n], in1=mhalf[:, 0:n], op=ALU.pow)
+            nc.gpsimd.tensor_tensor(out=st["rstd"][:], in0=var[:], in1=minus_half[:], op=ALU.pow)
 
-        def ln1(g):
+        def centre(g):
             if not ok(g):
                 return
             st = groups[g]
             st["o"] = work.tile([P, 2, WIDTH], F32, name="o%d" % g, tag="o", bufs=4)
-            for jj in range(plan[g][2]):
+            for jj in range(2):
                 nc.vector.scalar_tensor_tensor(
-                    out=st["o"][:, jj, :], in0=st["yc"][:, jj, :], scalar=st["nmu"][:, jj : jj + 1], in1=lnbank[:, 0:WIDTH],
-                    op0=ALU.add, op1=ALU.mult,
+                    out=st["o"][:, jj, :],
+                    in0=st["y"][:, jj, :],
+                    scalar=st["minus_mean"][:, jj : jj + 1],
+                    in1=ln_bank[:, 0:WIDTH],
+                    op0=ALU.add,
+                    op1=ALU.mult,
                 )
 
-        def ln2(g, split=False):
+        def finish(g):
             if not ok(g):
                 return
             st = groups[g]
-            s, j0, nj = plan[g]
-            rows = o_rows[s * SUPER : (s + 1) * SUPER, :].rearrange("(p j) d -> p j d", j=4)
-            for jj in range(nj):
+            s = g // 2
+            rows = out_rows[s * SUPER : (s + 1) * SUPER, :].rearrange("(p j) d -> p j d", j=4)
+            for jj in range(2):
                 nc.vector.scalar_tensor_tensor(
-                    out=st["o"][:, jj, :], in0=st["o"][:, jj, :], scalar=st["rs"][:, jj : jj + 1],
-                    in1=lnbank[:, WIDTH : 2 * WIDTH], op0=ALU.mult, op1=ALU.add,
+                    out=st["o"][:, jj, :],
+                    in0=st["o"][:, jj, :],
+                    scalar=st["rstd"][:, jj : jj + 1],
+                    in1=ln_bank[:, WIDTH : 2 * WIDTH],
+                    op0=ALU.mult,
+                    op1=ALU.add,
                 )
-                if split:
-                    nc.sync.dma_start(out=rows[:, j0 + jj : j0 + jj + 1, :], in_=st["o"][:, jj : jj + 1, :])
-            if not split:
-                nc.sync.dma_start(out=rows[:, j0 : j0 + nj, :], in_=st["o"][:, 0:nj, :])
+                j = 2 * (g % 2) + jj
+                nc.sync.dma_start(out=rows[:, j : j + 1, :], in_=st["o"][:, jj : jj + 1, :])
 
-        alloc(0)
-        w1raw = load_weight(attn_out_w, 0, "w1raw")
-        fetch(0, "c", 0, 2)
-        fetch(0, "x", 0, 2)
-        fetch(0, "q", 0, 2)
-        load_bias()
-        wgxraw = load_weight(gate_w, 0, "wgxraw")
-        fetch(0, "c", 2, 2)
-        wgqraw = load_weight(gate_w, 512, "wgqraw")
-        w2raw = load_weight(op_w, 0, "w2raw")
-        load_ln()
-        fetch(0, "x", 2, 2)
-        fetch(0, "q", 2, 2)
         loaded = 1
         for t in range(-2, N_GROUPS + 4):
             while loaded < N_SUPERS and 2 * loaded - 5 <= t:
-                load(loaded)
+                new_super(loaded)
+                for key in ("c", "x", "q"):
+                    fetch(loaded, key, 0, 4)
                 loaded += 1
             if t == -2:
-                prepare_weight(w1raw, "w1")
-            q_xq(t + 1)
-            q_rc(t)
+                prepare_weight(w1_raw, "w1")
+            quantise_xq(t + 1)
+            quantise_rc(t)
             if t == -1:
-                prepare_weight(wgxraw, "wgx")
-                prepare_weight(wgqraw, "wgq")
+                prepare_weight(wgx_raw, "wgx")
+                prepare_weight(wgq_raw, "wgq")
             if t == 0:
-                prepare_weight(w2raw, "w2")
-            if t == 1:
                 spread_ln()
-            tb(t - 3, 1)
-            ti(t + 2, "c")
+                prepare_weight(w2_raw, "w2")
+            blend(t - 3, 1)
+            turn(t + 2, "c")
             mean(t - 3)
-            ti(t + 2, "x")
-            if t < 2:
-                ti(t + 2, "q")
-            s2(t - 3)
-            pw(t - 3)
-            m2(t - 1)
-            m3(t)
-            sg(t)
-            sub(t - 1)
-            cm(t - 1, 0)
-            cm(t - 1, 1)
-            ln1(t - 3)
-            ln2(t - 4, t - 4 == N_GROUPS - 1)
-            tb(t - 2, 0)
-            if t >= 2:
-                ti(t + 2, "q")
+            deviation(t - 3)
+            turn(t + 2, "x")
+            if t < 3:
+                turn(t + 2, "q")
+            product_ret(t - 1)
+            product_gate(t)
+            subtract(t - 1)
+            multiply(t - 1)
+            centre(t - 3)
+            blend(t - 2, 0)
+            if t >= 3:
+                turn(t + 2, "q")
             if t == -2:
                 prepare_bias()
-            m1(t + 1)
+            product_r(t + 1)
+            finish(t - 4)

from contextlib import ExitStack

import concourse.mybir as mybir
from concourse.masks import make_identity

F32 = mybir.dt.float32
BF16 = mybir.dt.bfloat16
U32 = mybir.dt.uint32
U8 = mybir.dt.uint8
FP8X4 = mybir.dt.float8_e4m3fn_x4
ALU = mybir.AluOpType
ACT = mybir.ActivationFunctionType

P = 128
TOKENS = 4096
WIDTH = 512
SLOTS = 4
CHUNKS = WIDTH // P
GROUP = 2 * P
SUPER = 4 * P
N_GROUPS = TOKENS // GROUP
N_SUPERS = TOKENS // SUPER
LN_EPS = 1e-5
FLOPS = 2 * TOKENS * WIDTH * (512 + 512 + 1024)


def tile_rotelearningmemory_pa_t_kernel(
    tc, x, query, ctx, attn_out_w, attn_out_b, op_w, op_b, gate_w, gate_b, ln_g, ln_b, out
):
    nc = tc.nc
    sources = {"x": x.flatten_outer_dims(), "q": query.flatten_outer_dims(), "c": ctx.flatten_outer_dims()}
    out_rows = out.flatten_outer_dims()

    with ExitStack() as stack:
        stack.enter_context(tc.manual_schedule())
        const = stack.enter_context(tc.tile_pool(name="const", bufs=1))
        wtmp = stack.enter_context(tc.tile_pool(name="wtmp", bufs=2))
        raws = stack.enter_context(tc.tile_pool(name="raws", bufs=3))
        grps = stack.enter_context(tc.tile_pool(name="grps", bufs=3))
        cods = stack.enter_context(tc.tile_pool(name="cods", bufs=3))
        work = stack.enter_context(tc.tile_pool(name="work", bufs=3))
        stat = stack.enter_context(tc.tile_pool(name="stat", bufs=4))
        ln_pool = stack.enter_context(tc.psum_pool(name="ln_pool", bufs=1))
        banks = stack.enter_context(tc.psum_pool(name="banks", bufs=7))

        identf = const.tile([P, P], F32, name="identf")
        make_identity(nc, identf[:])
        identb = const.tile([P, P], BF16, name="identb")
        make_identity(nc, identb[:])
        minus_half = const.tile([P, 2], F32, name="minus_half")
        nc.gpsimd.memset(minus_half[:], -0.5)
        first_act = const.tile([P, 1], F32, name="first_act")
        nc.scalar.activation(out=first_act[:], in_=minus_half[:, 0:1], func=ACT.Sigmoid)
        squares = [const.tile([P, WIDTH], BF16, name="squares%d" % jj) for jj in range(2)]

        vectors = const.tile([P, WIDTH], BF16, name="vectors")
        nc.vector.memset(vectors[:], 0.0)
        ln_rows = const.tile([P, 2 * WIDTH], BF16, name="ln_rows")
        nc.vector.memset(ln_rows[:], 0.0)
        ones = const.tile([P, P], BF16, name="ones")
        nc.vector.memset(ones[:], 1.0)
        ln_bank = ln_pool.tile([P, 2 * WIDTH], BF16, name="ln_bank")

        supers = {}

        def new_super(s):
            supers[s] = {}
            for key, bufs in (("c", 3), ("x", 6), ("q", 3)):
                supers[s][key] = raws.tile([P, 4, WIDTH], BF16, name="%s%d" % (key, s), tag=key, bufs=bufs)

        def fetch(s, key, first, count):
            rows = sources[key][s * SUPER : (s + 1) * SUPER, :].rearrange("(p j) k -> p j k", j=4)
            part = slice(first, first + count)
            nc.sync.dma_start(out=supers[s][key][:, part, :], in_=rows[:, part, :])

        def load_weight(w, k0, name):
            raw = const.tile([P, SLOTS, WIDTH], BF16, name=name)
            nc.sync.dma_start(out=raw[:], in_=w.rearrange("(m t) k -> m t k", t=SLOTS)[:, :, k0 : k0 + WIDTH])
            return raw

        new_super(0)
        w1_raw = load_weight(attn_out_w, 0, "w1_raw")
        for key in ("c", "x", "q"):
            fetch(0, key, 0, 2)
        for row, vec in enumerate((attn_out_b, op_b, gate_b)):
            nc.sync.dma_start(out=vectors[row : row + 1, :], in_=vec.rearrange("(o w) -> o w", o=1))
        wgx_raw = load_weight(gate_w, 0, "wgx_raw")
        fetch(0, "c", 2, 2)
        wgq_raw = load_weight(gate_w, WIDTH, "wgq_raw")
        w2_raw = load_weight(op_w, 0, "w2_raw")
        for half, vec in enumerate((ln_g, ln_b)):
            cols = slice(half * WIDTH, (half + 1) * WIDTH)
            nc.sync.dma_start(out=ln_rows[0:1, cols], in_=vec.rearrange("(o d) -> o d", o=1))
        fetch(0, "x", 2, 2)
        fetch(0, "q", 2, 2)

        def transpose_words(bank, src, jj, u):
            col = u * GROUP + jj * P
            nc.tensor.transpose(bank[:, col : col + P], src.bitcast(F32)[:, u : 2 * P : 2], identf[:])

        def as_words(dst):
            return dst.bitcast(F32).rearrange("p (n u) -> p n u", u=2)

        def interleaved(bank):
            return bank[:].rearrange("p (u n) -> p n u", u=2)

        weights = {}

        def prepare_weight(raw, name):
            grp = wtmp.tile([P, SLOTS * WIDTH], BF16, name="grp_" + name, tag="wgrp", align_bytes=64)
            for half in range(2):
                bank = banks.tile([P, 512], F32, name="%s_%d" % (name, half), tag="bank")
                for jj in range(2):
                    for u in range(2):
                        transpose_words(bank, raw[:, 2 * half + jj, :], jj, u)
                cols = slice(half * SLOTS * GROUP, (half + 1) * SLOTS * GROUP)
                if half == 0:
                    nc.scalar.copy(out=as_words(grp[:, cols]), in_=interleaved(bank))
                else:
                    nc.vector.tensor_copy(out=as_words(grp[:, cols]), in_=interleaved(bank))
            codes = const.tile([P, WIDTH], U32, name="codes_" + name, align_bytes=64)
            scales = const.tile([P, WIDTH], U8, name="scales_" + name, align_bytes=64)
            nc.vector.quantize_mx(out=codes[:].bitcast(FP8X4), scales=scales[:], in_=grp[:])
            weights[name] = (codes, scales)

        bias = const.tile([P, 3 * CHUNKS], F32, name="bias")
        minus_gate_bias = const.tile([P, CHUNKS], F32, name="minus_gate_bias")

        def prepare_bias():
            bank = banks.tile([P, 512], F32, name="bias_bank", tag="bank")
            for u in range(2):
                transpose_words(bank, vectors[:], 0, u)
            words = const.tile([P, 8], F32, name="bias_words")
            nc.vector.tensor_copy(out=as_words(words[:, 0:6]), in_=interleaved(bank)[:, 0:3, :])
            nc.vector.tensor_copy(out=bias[:], in_=words[:, 0:6].bitcast(BF16))
            nc.vector.tensor_scalar(
                out=minus_gate_bias[:], in0=bias[:, 8:12], scalar1=-1.0, scalar2=None, op0=ALU.mult
            )

        def spread_ln():
            for half in range(2):
                cols = slice(half * WIDTH, (half + 1) * WIDTH)
                nc.tensor.matmul(out=ln_bank[:, cols], lhsT=ones[:], rhs=ln_rows[:, cols], start=True, stop=True)

        groups = [{} for g in range(N_GROUPS)]
        pairs = {}

        def ok(g):
            return 0 <= g < N_GROUPS

        def place(g, key):
            name = {"r": ("rc", g), "c": ("rc", g - 1), "x": ("xq", g), "q": ("xq", g)}[key]
            if name not in pairs:
                pairs[name] = {
                    "grp": grps.tile(
                        [P, 2 * SLOTS * GROUP],
                        BF16,
                        name="grp_%s%d" % (name[0], name[1] + 1),
                        tag=name[0],
                        bufs=(3 if name[0] == "rc" else 5),
                        align_bytes=64,
                    )
                }
            return pairs[name], (0 if key in ("r", "x") else 1)

        def grouped(g, key):
            pair, half = place(g, key)
            return pair["grp"][:, half * SLOTS * GROUP : (half + 1) * SLOTS * GROUP]

        def quantise(name, first, last):
            pair = pairs[name]
            label = "%s%d" % (name[0], name[1] + 1)
            pair["codes"] = cods.tile([P, 2 * GROUP], U32, name="codes_" + label, tag="codes_" + name[0], align_bytes=64)
            pair["scales"] = cods.tile([P, 2 * GROUP], U8, name="scales_" + label, tag="scales_" + name[0], align_bytes=64)
            cols = slice(first * GROUP, last * GROUP)
            nc.vector.quantize_mx(
                out=pair["codes"][:, cols].bitcast(FP8X4),
                scales=pair["scales"][:, cols],
                in_=pair["grp"][:, first * SLOTS * GROUP : last * SLOTS * GROUP],
            )

        def quantise_rc(g):
            first = 0 if ok(g) else 1
            last = 2 if ok(g + 1) else 1
            if first < last:
                quantise(("rc", g), first, last)

        def quantise_xq(g):
            if ok(g):
                quantise(("xq", g), 0, 2)

        def turn(g, key):
            if not ok(g):
                return
            bank = banks.tile([P, 512], F32, name="turn_%s%d" % (key, g), tag="bank")
            for jj in range(2):
                for u in range(2):
                    transpose_words(bank, supers[g // 2][key][:, 2 * (g % 2) + jj, :], jj, u)
            nc.scalar.copy(out=as_words(grouped(g, key)), in_=interleaved(bank))

        def mx(dst, weight, c, g, key, first, count, start, stop):
            codes, scales = weights[weight]
            pair, half = place(g, key)
            channels = slice(c * P, (c + 1) * P)
            tokens = slice(half * GROUP + first, half * GROUP + first + count)
            nc.tensor.matmul_mx(
                out=dst,
                lhsT=codes[:, channels].bitcast(FP8X4),
                lhsT_scale=scales[:, channels],
                rhs=pair["codes"][:, tokens].bitcast(FP8X4),
                rhs_scale=pair["scales"][:, tokens],
                start=start,
                stop=stop,
            )

        def product_r(g):
            if not ok(g):
                return
            for jj in range(2):
                bank = banks.tile([P, 512], F32, name="r%d_%d" % (g, jj), tag="bank")
                for c in range(CHUNKS):
                    mx(bank[:, c * P : (c + 1) * P], "w1", c, g, "c", jj * P, P, True, True)
                nc.vector.tensor_tensor(
                    out=grouped(g, "r").rearrange("p (n c) -> p n c", c=CHUNKS)[:, jj * P : (jj + 1) * P, :],
                    in0=bank[:].rearrange("p (c n) -> p n c", c=CHUNKS),
                    in1=bias[:, 0:4].unsqueeze(1).to_broadcast([P, P, CHUNKS]),
                    op=ALU.add,
                )

        def chunk_of(two_banks, c):
            return two_banks[c // 2][:, (c % 2) * GROUP : (c % 2 + 1) * GROUP]

        def product_ret(g):
            if not ok(g):
                return
            groups[g]["ret"] = [banks.tile([P, 512], F32, name="ret%d_%d" % (g, b), tag="bank") for b in range(2)]
            for c in range(CHUNKS):
                mx(chunk_of(groups[g]["ret"], c), "w2", c, g, "r", 0, GROUP, True, True)

        def product_gate(g):
            if not ok(g):
                return
            st = groups[g]
            st["h"] = work.tile([P, CHUNKS, GROUP], F32, name="h%d" % g, tag="h", bufs=4)
            gate = [banks.tile([P, 512], F32, name="gate%d_%d" % (g, b), tag="bank") for b in range(2)]
            for c in range(CHUNKS):
                mx(chunk_of(gate, c), "wgx", c, g, "x", 0, GROUP, True, False)
                mx(chunk_of(gate, c), "wgq", c, g, "q", 0, GROUP, False, True)
            for c in range(CHUNKS):
                nc.scalar.activation(
                    out=st["h"][:, c, :],
                    in_=chunk_of(gate, c),
                    func=ACT.Sigmoid,
                    bias=minus_gate_bias[:, c : c + 1],
                    scale=-1.0,
                )

        def subtract(g):
            if not ok(g):
                return
            st = groups[g]
            st["d"] = work.tile([P, CHUNKS, GROUP], F32, name="d%d" % g, tag="d", bufs=5)
            for c in range(CHUNKS):
                nc.vector.scalar_tensor_tensor(
                    out=st["d"][:, c, :],
                    in0=chunk_of(st["ret"], c),
                    scalar=bias[:, 4 + c : 5 + c],
                    in1=grouped(g, "x").rearrange("p (n t) -> p n t", t=SLOTS)[:, :, c],
                    op0=ALU.add,
                    op1=ALU.subtract,
                )

        def multiply(g):
            if not ok(g):
                return
            st = groups[g]
            for jj in range(2):
                tile = slice(jj * P, (jj + 1) * P)
                nc.gpsimd.tensor_tensor(
                    out=st["d"][:, :, tile], in0=st["d"][:, :, tile], in1=st["h"][:, :, tile], op=ALU.mult
                )

        def blend(g, jj):
            if not ok(g):
                return
            st = groups[g]
            if jj == 0:
                st["y"] = work.tile([P, 2, WIDTH], F32, name="y%d" % g, tag="y")
                for key in ("sum", "minus_mean", "sum_squares"):
                    st[key] = stat.tile([P, 2], F32, name="%s%d" % (key, g), tag=key)
            bank = banks.tile([P, 512], F32, name="y%d_%d" % (g, jj), tag="bank")
            nc.tensor.matmul(
                out=bank[:], lhsT=identb[:], rhs=supers[g // 2]["x"][:, 2 * (g % 2) + jj, :], start=True, stop=False
            )
            for c in range(CHUNKS):
                nc.tensor.matmul(
                    out=bank[:].rearrange("p (m t) -> p m t", t=SLOTS)[:, :, c],
                    lhsT=st["d"][:, c, jj * P : (jj + 1) * P],
                    rhs=identf[:],
                    is_transpose=True,
                    start=False,
                    stop=(c == CHUNKS - 1),
                )
            nc.scalar.activation(
                out=st["y"][:, jj, :], in_=bank[:], func=ACT.Identity, accum_out=st["sum"][:, jj : jj + 1]
            )

        def mean(g):
            if ok(g):
                nc.scalar.mul(out=groups[g]["minus_mean"][:], in_=groups[g]["sum"][:], mul=-1.0 / WIDTH)

        def deviation(g):
            if not ok(g):
                return
            st = groups[g]
            for jj in range(2):
                nc.scalar.activation(
                    out=squares[jj][:],
                    in_=st["y"][:, jj, :],
                    func=ACT.Square,
                    bias=st["minus_mean"][:, jj : jj + 1],
                    scale=1.0,
                    accum_out=st["sum_squares"][:, jj : jj + 1],
                )
            var = stat.tile([P, 2], F32, name="var%d" % g, tag="var")
            st["rstd"] = stat.tile([P, 2], F32, name="rstd%d" % g, tag="rstd")
            nc.gpsimd.tensor_scalar(
                out=var[:], in0=st["sum_squares"][:], scalar1=1.0 / WIDTH, scalar2=LN_EPS, op0=ALU.mult, op1=ALU.add
            )
            nc.gpsimd.tensor_tensor(out=st["rstd"][:], in0=var[:], in1=minus_half[:], op=ALU.pow)

        def centre(g):
            if not ok(g):
                return
            st = groups[g]
            st["o"] = work.tile([P, 2, WIDTH], F32, name="o%d" % g, tag="o", bufs=4)
            for jj in range(2):
                nc.vector.scalar_tensor_tensor(
                    out=st["o"][:, jj, :],
                    in0=st["y"][:, jj, :],
                    scalar=st["minus_mean"][:, jj : jj + 1],
                    in1=ln_bank[:, 0:WIDTH],
                    op0=ALU.add,
                    op1=ALU.mult,
                )

        def finish(g):
            if not ok(g):
                return
            st = groups[g]
            s = g // 2
            rows = out_rows[s * SUPER : (s + 1) * SUPER, :].rearrange("(p j) d -> p j d", j=4)
            for jj in range(2):
                nc.vector.scalar_tensor_tensor(
                    out=st["o"][:, jj, :],
                    in0=st["o"][:, jj, :],
                    scalar=st["rstd"][:, jj : jj + 1],
                    in1=ln_bank[:, WIDTH : 2 * WIDTH],
                    op0=ALU.mult,
                    op1=ALU.add,
                )
                j = 2 * (g % 2) + jj
                nc.sync.dma_start(out=rows[:, j : j + 1, :], in_=st["o"][:, jj : jj + 1, :])

        loaded = 1
        for t in range(-2, N_GROUPS + 4):
            while loaded < N_SUPERS and 2 * loaded - 5 <= t:
                new_super(loaded)
                for key in ("c", "x", "q"):
                    fetch(loaded, key, 0, 4)
                loaded += 1
            if t == -2:
                prepare_weight(w1_raw, "w1")
            quantise_xq(t + 1)
            quantise_rc(t)
            if t == -1:
                prepare_weight(wgx_raw, "wgx")
                prepare_weight(wgq_raw, "wgq")
            if t == 0:
                spread_ln()
                prepare_weight(w2_raw, "w2")
            blend(t - 3, 1)
            turn(t + 2, "c")
            mean(t - 3)
            deviation(t - 3)
            turn(t + 2, "x")
            if t < 3:
                turn(t + 2, "q")
            product_ret(t - 1)
            product_gate(t)
            subtract(t - 1)
            multiply(t - 1)
            centre(t - 3)
            blend(t - 2, 0)
            if t >= 3:
                turn(t + 2, "q")
            if t == -2:
                prepare_bias()
            product_r(t + 1)
            finish(t - 4)
